import numpy as np
import ml_dtypes


def mxq(x, axis, fmt="e4m3"):
    dtype, down = {"e4m3": (ml_dtypes.float8_e4m3fn, 7), "e5m2": (ml_dtypes.float8_e5m2, 14)}[fmt]
    v = np.moveaxis(np.asarray(x, np.float32).astype(ml_dtypes.bfloat16).astype(np.float64), axis, -1)
    blocks = v.reshape(v.shape[:-1] + (-1, 32))
    amax = np.abs(blocks).max(-1, keepdims=True)
    byte = np.maximum(np.where(amax > 0, np.frexp(amax)[1] - 1 + 127, 0) - down, 1)
    scale = np.exp2(byte - 127.0)
    codes = (blocks / scale).astype(np.float32).astype(dtype).astype(np.float64)
    return np.moveaxis((codes * scale).reshape(v.shape), -1, axis)


WIDE = False


def mx_kscale(k):
    if not WIDE:
        return np.ones(k)
    levels = np.array([10, -10, 5, -5, 0])
    a = np.random.permutation(np.resize(levels, k // 512 * 4)).reshape(k // 512, 4)
    idx = np.arange(k)
    return np.exp2(a[idx // 512, idx % 128 // 32])


BF16 = ml_dtypes.bfloat16


def bf(x):
    return np.asarray(x, np.float32).astype(BF16)


def f64(x):
    return np.asarray(x).astype(np.float64)


B, K, G, D, FF, F, P, H = 128, 32, 128, 1024, 512, 2048, 7, 8
NC = K * G
EPS = 1e-5


def layernorm(x, g, b):
    m = x.mean(-1, keepdims=True)
    v = ((x - m) ** 2).mean(-1, keepdims=True)
    return (x - m) / np.sqrt(v + EPS) * g + b


def setup_inputs():
    n = np.random.standard_normal
    s, t = mx_kscale(FF), mx_kscale(D)
    return {
        "ff_hid": bf(np.maximum(n((B, K, FF)), 0.0) * s),
        "tgt": bf(n((B, K, D))),
        "w2": bf(n((FF, D)) / np.sqrt(FF) / s[:, None]),
        "b2": bf(0.1 * n(D)),
        "g3": bf((1.0 + 0.1 * n(D)) * t),
        "be3": bf(0.1 * n(D) * t),
        "dup_pool": bf(n((K, D, G)) / np.sqrt(D) / t[None, :, None]),
        "dup_bias": bf(0.2 * n(NC)),
    }


def reference(ff_hid, tgt, w2, b2, g3, be3, dup_pool, dup_bias):
    ff = (mxq(f64(ff_hid), 2, "e4m3") @ mxq(f64(w2), 0, "e4m3")) + f64(b2)
    h = layernorm(f64(tgt) + ff, f64(g3), f64(be3))
    out_extrap = (mxq(h, 2, "e4m3").transpose(1, 0, 2) @ mxq(f64(dup_pool), 1, "e4m3")).transpose(1, 0, 2)
    return out_extrap.reshape(B, -1)[:, :NC] + f64(dup_bias)

@@ -1,0 +1,214 @@
+from contextlib import ExitStack
+
+import concourse.bass as bass
+import concourse.mybir as mybir
+import concourse.tile as tile
+from concourse.masks import make_identity
+
+F32 = mybir.dt.float32
+BF16 = mybir.dt.bfloat16
+U32 = mybir.dt.uint32
+U8 = mybir.dt.uint8
+FP8X4 = mybir.dt.float8_e4m3fn_x4
+ALU = mybir.AluOpType
+ACT = mybir.ActivationFunctionType
+
+P = 128
+B, K, G, D, FF = 128, 32, 128, 1024, 512
+EPS = 1e-5
+FLOPS = 2 * B * K * FF * D + 2 * B * K * D * G
+
+XHAT_ON_SCALAR = True
+AFFINE_ON_VECTOR_EVERY = 0
+
+
+def tile_mldecoder_pb_t_kernel(tc, ff_hid, tgt, w2, b2, g3, be3, dup_pool, dup_bias, out):
+    nc = tc.nc
+    with ExitStack() as ctx:
+        const = ctx.enter_context(tc.tile_pool(name="const", bufs=1))
+        loads = ctx.enter_context(tc.tile_pool(name="loads", bufs=3))
+        work = ctx.enter_context(tc.tile_pool(name="work", bufs=3))
+        small = ctx.enter_context(tc.tile_pool(name="small", bufs=6))
+        psum = ctx.enter_context(tc.psum_pool(name="psum", bufs=1))
+
+        eps_t = const.tile([P, 1], F32)
+        nc.vector.memset(eps_t[:], EPS)
+        warm = const.tile([P, 1], F32)
+        nc.scalar.activation(out=warm[:], in_=eps_t[:], func=ACT.Sqrt)
+        ident_f = const.tile([P, P], F32)
+        make_identity(nc, ident_f[:])
+        ident_b = const.tile([P, P], BF16)
+        make_identity(nc, ident_b[:])
+
+        w2raw = const.tile([P, 4, D], BF16)
+        for u in range(2):
+            nc.sync.dma_start(
+                out=w2raw[:, 2 * u : 2 * u + 2, :],
+                in_=w2[256 * u : 256 * u + 256, :].rearrange("(q e) c -> q e c", e=2),
+            )
+        b2bc = const.tile([P, D], BF16)
+        nc.sync.dma_start(out=b2bc[:], in_=b2.partition_broadcast(P))
+
+        gb_raw = const.tile([P, P], BF16)
+        nc.vector.memset(gb_raw[:], 0.0)
+        nc.sync.dma_start(out=gb_raw[0:8, :], in_=g3.rearrange("(c p) -> c p", p=P))
+        nc.sync.dma_start(out=gb_raw[8:16, :], in_=be3.rearrange("(c p) -> c p", p=P))
+
+        w2c = const.tile([P, D], U32, align_bytes=64)
+        w2s = const.tile([P, D], U8, align_bytes=64)
+        w2g = const.tile([P, 2, 512, 4], BF16, align_bytes=64)
+        for h in range(2):
+            nc.vector.tensor_copy(
+                out=w2g[:, h], in_=w2raw[:, :, 512 * h : 512 * h + 512].rearrange("p t c -> p c t")
+            )
+        for h in range(2):
+            nc.vector.quantize_mx(
+                out=w2c[:, 512 * h : 512 * h + 512].bitcast(FP8X4),
+                scales=w2s[:, 512 * h : 512 * h + 512],
+                in_=w2g[:, h].rearrange("p c t -> p (c t)"),
+            )
+
+        gb_ps = psum.tile([P, P], BF16, tag="ffT", bufs=1)
+        nc.tensor.transpose(gb_ps[:], gb_raw[:], ident_b[:])
+        gb = const.tile([P, 16], F32)
+        nc.vector.tensor_copy(out=gb[:], in_=gb_ps[:, 0:16])
+
+        dbias = const.tile([P, K * G], BF16)
+
+        ffh_t = {}
+        tgt_t = {}
+        dup_t = {}
+        ff_q = {}
+        o2_t = {}
+
+        for k in range(K):
+            if k % 8 == 0:
+                ffh = loads.tile([P, 8, FF], BF16, tag="ffh", bufs=4)
+                nc.sync.dma_start(out=ffh[:], in_=ff_hid[:, k : k + 8, :])
+                ffh_t[k // 8] = ffh
+            if k % 4 == 0:
+                tg = loads.tile([P, 4, D], BF16, tag="tg", bufs=3)
+                nc.sync.dma_start(out=tg[:], in_=tgt[:, k : k + 4, :])
+                tgt_t[k // 4] = tg
+                dr = loads.tile([P, 4, 8, G], BF16, tag="dr", bufs=3)
+                nc.sync.dma_start(out=dr[:], in_=dup_pool[k : k + 4].rearrange("k (c p) g -> p k c g", p=P))
+                dup_t[k // 4] = dr
+            if k == 0:
+                nc.sync.dma_start(out=dbias[:], in_=dup_bias.partition_broadcast(P))
+
+            if k % 2 == 0:
+                ffT = psum.tile([P, 2, 2, P], F32, tag="ffT", bufs=1)
+                for j in range(2):
+                    words = ffh_t[k // 8][:, (k + j) % 8, :].bitcast(F32)
+                    for u in range(2):
+                        nc.tensor.transpose(ffT[:, j, u, :], words[:, P * u : P * u + P], ident_f[:])
+                ffg = work.tile([P, 2, P, 4], BF16, tag="ffg", bufs=2, align_bytes=64)
+                nc.scalar.copy(out=ffg[:].bitcast(F32), in_=ffT[:].rearrange("p j u b -> p j b u"))
+                ffc = work.tile([P, 2 * P], U32, tag="ffc", bufs=3, align_bytes=64)
+                ffs = work.tile([P, 2 * P], U8, tag="ffs", bufs=3, align_bytes=64)
+                nc.vector.quantize_mx(
+                    out=ffc[:].bitcast(FP8X4), scales=ffs[:], in_=ffg[:].rearrange("p j b t -> p (j b t)")
+                )
+                ff_q[k // 2] = (ffc, ffs)
+
+            u_t = work.tile([P, D], F32, tag="u", bufs=4)
+            nc.vector.tensor_tensor(out=u_t[:], in0=tgt_t[k // 4][:, k % 4, :], in1=b2bc[:], op=ALU.add)
+
+            ffc, ffs = ff_q[k // 2]
+            cols = slice(P * (k % 2), P * (k % 2) + P)
+            s0 = small.tile([P, 2], F32, tag="s0")
+            for h in range(2):
+                s1 = psum.tile([P, 512], F32, tag="s1", bufs=4)
+                n_cols = slice(512 * h, 512 * h + 512)
+                nc.tensor.matmul_mx(
+                    out=s1[:],
+                    lhsT=ffc[:, cols].bitcast(FP8X4),
+                    lhsT_scale=ffs[:, cols],
+                    rhs=w2c[:, n_cols].bitcast(FP8X4),
+                    rhs_scale=w2s[:, n_cols],
+                    start=True,
+                    stop=True,
+                )
+                nc.vector.scalar_tensor_tensor(
+                    out=u_t[:, n_cols],
+                    in0=s1[:],
+                    scalar=1.0,
+                    in1=u_t[:, n_cols],
+                    op0=ALU.mult,
+                    op1=ALU.add,
+                    accum_out=s0[:, h : h + 1],
+                )
+            negm = small.tile([P, 1], F32, tag="negm")
+            nc.vector.tensor_scalar(
+                out=negm[:], in0=s0[:, 0:1], scalar1=s0[:, 1:2], scalar2=-1.0 / D, op0=ALU.add, op1=ALU.mult
+            )
+            junk = work.tile([P, D], BF16, tag="junk", bufs=2)
+            ss = small.tile([P, 1], F32, tag="ss")
+            nc.scalar.activation(out=junk[:], in_=u_t[:], func=ACT.Square, bias=negm[:], scale=1.0, accum_out=ss[:])
+            std = small.tile([P, 1], F32, tag="std")
+            nc.scalar.activation(out=std[:], in_=ss[:], func=ACT.Sqrt, bias=eps_t[:], scale=1.0 / D)
+            rstd = small.tile([P, 1], F32, tag="rstd")
+            nc.vector.reciprocal(out=rstd[:], in_=std[:])
+
+            z = work.tile([P, D], F32, tag="z", bufs=3)
+            if XHAT_ON_SCALAR:
+                nb = small.tile([P, 1], F32, tag="nb")
+                nc.vector.tensor_tensor(out=nb[:], in0=negm[:], in1=rstd[:], op=ALU.mult)
+                nc.scalar.activation(out=z[:], in_=u_t[:], func=ACT.Identity, bias=nb[:], scale=rstd[:])
+            else:
+                nc.vector.tensor_scalar(
+                    out=z[:], in0=u_t[:], scalar1=negm[:], scalar2=rstd[:], op0=ALU.add, op1=ALU.mult
+                )
+
+            hp = work.tile([P, 8, P], BF16, tag="hp", bufs=3)
+            for a in range(2):
+                zT = psum.tile([P, 4, P], F32, tag="zT", bufs=2)
+                for t in range(4):
+                    c = 4 * a + t
+                    nc.tensor.transpose(zT[:, t, :], z[:, P * c : P * c + P], ident_f[:])
+                bank = 2 * k + a
+                on_vector = AFFINE_ON_VECTOR_EVERY > 0 and bank % AFFINE_ON_VECTOR_EVERY == 0
+                for t in range(4):
+                    c = 4 * a + t
+                    if on_vector:
+                        nc.vector.tensor_scalar(
+                            out=hp[:, c, :], in0=zT[:, t, :], scalar1=gb[:, c : c + 1],
+                            scalar2=gb[:, 8 + c : 9 + c], op0=ALU.mult, op1=ALU.add,
+                        )
+                    else:
+                        nc.scalar.activation(
+                            out=hp[:, c, :], in_=zT[:, t, :], func=ACT.Identity,
+                            bias=gb[:, 8 + c : 9 + c], scale=gb[:, c : c + 1],
+                        )
+            hg = work.tile([P, 2, P, 4], BF16, tag="hg", bufs=3, align_bytes=64)
+            nc.vector.tensor_copy(out=hg[:], in_=hp[:].rearrange("p (a t) b -> p a b t", t=4))
+            hc = work.tile([P, 2 * P], U32, tag="hc", bufs=3, align_bytes=64)
+            hs = work.tile([P, 2 * P], U8, tag="hs", bufs=3, align_bytes=64)
+            nc.vector.quantize_mx(out=hc[:].bitcast(FP8X4), scales=hs[:], in_=hg[:].rearrange("p a b t -> p (a b t)"))
+
+            dg = work.tile([P, 2, G, 4], BF16, tag="dg", bufs=3, align_bytes=64)
+            nc.vector.tensor_copy(out=dg[:], in_=dup_t[k // 4][:, k % 4].rearrange("p (a t) g -> p a g t", t=4))
+            dc = work.tile([P, 2 * G], U32, tag="dc", bufs=3, align_bytes=64)
+            ds = work.tile([P, 2 * G], U8, tag="ds", bufs=3, align_bytes=64)
+            nc.vector.quantize_mx(out=dc[:].bitcast(FP8X4), scales=ds[:], in_=dg[:].rearrange("p a g t -> p (a g t)"))
+
+            if k % 4 == 0:
+                o2 = psum.tile([P, 4 * G], F32, tag="o2", bufs=1)
+                o2_t[k // 4] = o2
+            o2 = o2_t[k // 4]
+            for a in range(2):
+                sl = slice(P * a, P * a + P)
+                nc.tensor.matmul_mx(
+                    out=o2[:, G * (k % 4) : G * (k % 4) + G],
+                    lhsT=hc[:, sl].bitcast(FP8X4),
+                    lhsT_scale=hs[:, sl],
+                    rhs=dc[:, sl].bitcast(FP8X4),
+                    rhs_scale=ds[:, sl],
+                    start=(a == 0),
+                    stop=(a == 1),
+                )
+            if k % 4 == 3:
+                o_cols = slice(G * (k - 3), G * (k + 1))
+                ob = work.tile([P, 4 * G], F32, tag="ob", bufs=3)
+                nc.vector.tensor_tensor(out=ob[:], in0=o2[:], in1=dbias[:, o_cols], op=ALU.add)
+                nc.sync.dma_start(out=out[:, o_cols], in_=ob[:])

@@ -1,8 +1,6 @@
 from contextlib import ExitStack
 
-import concourse.bass as bass
 import concourse.mybir as mybir
-import concourse.tile as tile
 from concourse.masks import make_identity
 
 F32 = mybir.dt.float32
@@ -17,9 +15,7 @@ P = 128
 B, K, G, D, FF = 128, 32, 128, 1024, 512
 EPS = 1e-5
 FLOPS = 2 * B * K * FF * D + 2 * B * K * D * G
-
-XHAT_ON_SCALAR = True
-AFFINE_ON_VECTOR_EVERY = 0
+NG = K // 4
 
 
 def tile_mldecoder_pb_t_kernel(tc, ff_hid, tgt, w2, b2, g3, be3, dup_pool, dup_bias, out):
@@ -31,10 +27,8 @@ def tile_mldecoder_pb_t_kernel(tc, ff_hid, tgt, w2, b2, g3, be3, dup_pool, dup_b
         small = ctx.enter_context(tc.tile_pool(name="small", bufs=6))
         psum = ctx.enter_context(tc.psum_pool(name="psum", bufs=1))
 
-        eps_t = const.tile([P, 1], F32)
-        nc.vector.memset(eps_t[:], EPS)
-        warm = const.tile([P, 1], F32)
-        nc.scalar.activation(out=warm[:], in_=eps_t[:], func=ACT.Sqrt)
+        mhalf = const.tile([P, 1], F32)
+        nc.vector.memset(mhalf[:], -0.5)
         ident_f = const.tile([P, P], F32)
         make_identity(nc, ident_f[:])
         ident_b = const.tile([P, P], BF16)
@@ -46,20 +40,41 @@ def tile_mldecoder_pb_t_kernel(tc, ff_hid, tgt, w2, b2, g3, be3, dup_pool, dup_b
                 out=w2raw[:, 2 * u : 2 * u + 2, :],
                 in_=w2[256 * u : 256 * u + 256, :].rearrange("(q e) c -> q e c", e=2),
             )
-        b2bc = const.tile([P, D], BF16)
-        nc.sync.dma_start(out=b2bc[:], in_=b2.partition_broadcast(P))
-
         gb_raw = const.tile([P, P], BF16)
         nc.vector.memset(gb_raw[:], 0.0)
         nc.sync.dma_start(out=gb_raw[0:8, :], in_=g3.rearrange("(c p) -> c p", p=P))
         nc.sync.dma_start(out=gb_raw[8:16, :], in_=be3.rearrange("(c p) -> c p", p=P))
+        nc.sync.dma_start(out=gb_raw[16:24, :], in_=b2.rearrange("(c p) -> c p", p=P))
+
+        ffh_t = {}
+        tgt_t = {}
+        dup_t = {}
+
+        def load_ffh(i):
+            ffh = loads.tile([P, 8, FF], BF16, tag="ffh", bufs=4)
+            nc.sync.dma_start(out=ffh[:], in_=ff_hid[:, 8 * i : 8 * i + 8, :])
+            ffh_t[i] = ffh
+
+        def load_group(g):
+            tg = loads.tile([P, 4, D], BF16, tag="tg", bufs=3)
+            nc.sync.dma_start(out=tg[:], in_=tgt[:, 4 * g : 4 * g + 4, :])
+            tgt_t[g] = tg
+            dr = loads.tile([P, 4, 8, G], BF16, tag="dr", bufs=3)
+            nc.sync.dma_start(out=dr[:], in_=dup_pool[4 * g : 4 * g + 4].rearrange("k (c p) g -> p k c g", p=P))
+            dup_t[g] = dr
+
+        load_ffh(0)
+        load_group(0)
+        dbias = const.tile([P, K * G], BF16)
+        nc.sync.dma_start(out=dbias[:], in_=dup_bias.partition_broadcast(P))
 
         w2c = const.tile([P, D], U32, align_bytes=64)
         w2s = const.tile([P, D], U8, align_bytes=64)
         w2g = const.tile([P, 2, 512, 4], BF16, align_bytes=64)
         for h in range(2):
             nc.vector.tensor_copy(
-                out=w2g[:, h], in_=w2raw[:, :, 512 * h : 512 * h + 512].rearrange("p t c -> p c t")
+                out=w2g[:, h].rearrange("p (c i) t -> p c t i", i=4),
+                in_=w2raw[:, :, 512 * h : 512 * h + 512].rearrange("p t (c i) -> p c t i", i=4),
             )
         for h in range(2):
             nc.vector.quantize_mx(
@@ -68,138 +83,125 @@ def tile_mldecoder_pb_t_kernel(tc, ff_hid, tgt, w2, b2, g3, be3, dup_pool, dup_b
                 in_=w2g[:, h].rearrange("p c t -> p (c t)"),
             )
 
-        gb_ps = psum.tile([P, P], BF16, tag="ffT", bufs=1)
+        gb_ps = psum.tile([P, P], BF16, tag="ffhT", bufs=1)
         nc.tensor.transpose(gb_ps[:], gb_raw[:], ident_b[:])
-        gb = const.tile([P, 16], F32)
-        nc.vector.tensor_copy(out=gb[:], in_=gb_ps[:, 0:16])
+        gb = const.tile([P, 24], F32)
+        nc.vector.tensor_copy(out=gb[:], in_=gb_ps[:, 0:24])
 
-        dbias = const.tile([P, K * G], BF16)
-
-        ffh_t = {}
-        tgt_t = {}
-        dup_t = {}
         ff_q = {}
+        ffb_t = {}
         o2_t = {}
+        st = {}
 
-        for k in range(K):
-            if k % 8 == 0:
-                ffh = loads.tile([P, 8, FF], BF16, tag="ffh", bufs=4)
-                nc.sync.dma_start(out=ffh[:], in_=ff_hid[:, k : k + 8, :])
-                ffh_t[k // 8] = ffh
-            if k % 4 == 0:
-                tg = loads.tile([P, 4, D], BF16, tag="tg", bufs=3)
-                nc.sync.dma_start(out=tg[:], in_=tgt[:, k : k + 4, :])
-                tgt_t[k // 4] = tg
-                dr = loads.tile([P, 4, 8, G], BF16, tag="dr", bufs=3)
-                nc.sync.dma_start(out=dr[:], in_=dup_pool[k : k + 4].rearrange("k (c p) g -> p k c g", p=P))
-                dup_t[k // 4] = dr
-            if k == 0:
-                nc.sync.dma_start(out=dbias[:], in_=dup_bias.partition_broadcast(P))
-
-            if k % 2 == 0:
-                ffT = psum.tile([P, 2, 2, P], F32, tag="ffT", bufs=1)
+        def ff_prep(g):
+            ffc = work.tile([P, 4 * P], U32, tag="ffc", bufs=2, align_bytes=64)
+            ffs = work.tile([P, 4 * P], U8, tag="ffs", bufs=2, align_bytes=64)
+            for pair in range(2):
+                ffhT = psum.tile([P, 2, 2, P], F32, tag="ffhT", bufs=1)
                 for j in range(2):
-                    words = ffh_t[k // 8][:, (k + j) % 8, :].bitcast(F32)
+                    k = 4 * g + 2 * pair + j
+                    words = ffh_t[k // 8][:, k % 8, :].bitcast(F32)
                     for u in range(2):
-                        nc.tensor.transpose(ffT[:, j, u, :], words[:, P * u : P * u + P], ident_f[:])
+                        nc.tensor.transpose(ffhT[:, j, u, :], words[:, P * u : P * u + P], ident_f[:])
                 ffg = work.tile([P, 2, P, 4], BF16, tag="ffg", bufs=2, align_bytes=64)
-                nc.scalar.copy(out=ffg[:].bitcast(F32), in_=ffT[:].rearrange("p j u b -> p j b u"))
-                ffc = work.tile([P, 2 * P], U32, tag="ffc", bufs=3, align_bytes=64)
-                ffs = work.tile([P, 2 * P], U8, tag="ffs", bufs=3, align_bytes=64)
+                nc.scalar.copy(out=ffg[:].bitcast(F32), in_=ffhT[:].rearrange("p j u b -> p j b u"))
+                sl = slice(2 * P * pair, 2 * P * pair + 2 * P)
                 nc.vector.quantize_mx(
-                    out=ffc[:].bitcast(FP8X4), scales=ffs[:], in_=ffg[:].rearrange("p j b t -> p (j b t)")
+                    out=ffc[:, sl].bitcast(FP8X4), scales=ffs[:, sl], in_=ffg[:].rearrange("p j b t -> p (j b t)")
                 )
-                ff_q[k // 2] = (ffc, ffs)
+            ff_q[g] = (ffc, ffs)
 
+        def mx_chunk(g, c):
+            ffc, ffs = ff_q[g]
+            mm = psum.tile([P, 4 * P], F32, tag="mm", bufs=2)
+            sl = slice(P * c, P * c + P)
+            nc.tensor.matmul_mx(
+                out=mm[:],
+                lhsT=w2c[:, sl].bitcast(FP8X4),
+                lhsT_scale=w2s[:, sl],
+                rhs=ffc[:].bitcast(FP8X4),
+                rhs_scale=ffs[:],
+                start=True,
+                stop=True,
+            )
+            ffb = work.tile([P, 4 * P], F32, tag="ffb", bufs=16)
+            nc.scalar.activation(out=ffb[:], in_=mm[:], func=ACT.Identity, bias=gb[:, 16 + c : 17 + c], scale=1.0)
+            ffb_t[(g, c)] = ffb
+
+        def front(k):
+            g, j = divmod(k, 4)
             u_t = work.tile([P, D], F32, tag="u", bufs=4)
-            nc.vector.tensor_tensor(out=u_t[:], in0=tgt_t[k // 4][:, k % 4, :], in1=b2bc[:], op=ALU.add)
-
-            ffc, ffs = ff_q[k // 2]
-            cols = slice(P * (k % 2), P * (k % 2) + P)
             s0 = small.tile([P, 2], F32, tag="s0")
             for h in range(2):
-                s1 = psum.tile([P, 512], F32, tag="s1", bufs=4)
+                s1 = psum.tile([P, 4, P], F32, tag="s1", bufs=2)
+                for t in range(4):
+                    nc.tensor.transpose(s1[:, t, :], ffb_t[(g, 4 * h + t)][:, P * j : P * j + P], ident_f[:])
                 n_cols = slice(512 * h, 512 * h + 512)
-                nc.tensor.matmul_mx(
-                    out=s1[:],
-                    lhsT=ffc[:, cols].bitcast(FP8X4),
-                    lhsT_scale=ffs[:, cols],
-                    rhs=w2c[:, n_cols].bitcast(FP8X4),
-                    rhs_scale=w2s[:, n_cols],
-                    start=True,
-                    stop=True,
-                )
                 nc.vector.scalar_tensor_tensor(
                     out=u_t[:, n_cols],
-                    in0=s1[:],
+                    in0=s1[:].rearrange("p t d -> p (t d)"),
                     scalar=1.0,
-                    in1=u_t[:, n_cols],
+                    in1=tgt_t[g][:, j, n_cols],
                     op0=ALU.mult,
                     op1=ALU.add,
                     accum_out=s0[:, h : h + 1],
                 )
             negm = small.tile([P, 1], F32, tag="negm")
-            nc.vector.tensor_scalar(
+            nc.gpsimd.tensor_scalar(
                 out=negm[:], in0=s0[:, 0:1], scalar1=s0[:, 1:2], scalar2=-1.0 / D, op0=ALU.add, op1=ALU.mult
             )
             junk = work.tile([P, D], BF16, tag="junk", bufs=2)
             ss = small.tile([P, 1], F32, tag="ss")
             nc.scalar.activation(out=junk[:], in_=u_t[:], func=ACT.Square, bias=negm[:], scale=1.0, accum_out=ss[:])
-            std = small.tile([P, 1], F32, tag="std")
-            nc.scalar.activation(out=std[:], in_=ss[:], func=ACT.Sqrt, bias=eps_t[:], scale=1.0 / D)
+            ve = small.tile([P, 1], F32, tag="ve")
+            nc.gpsimd.tensor_scalar(out=ve[:], in0=ss[:], scalar1=1.0 / D, scalar2=EPS, op0=ALU.mult, op1=ALU.add)
             rstd = small.tile([P, 1], F32, tag="rstd")
-            nc.vector.reciprocal(out=rstd[:], in_=std[:])
+            nc.gpsimd.tensor_tensor(out=rstd[:], in0=ve[:], in1=mhalf[:], op=ALU.pow)
+            st[k] = (u_t, negm, rstd)
 
+        def back(k):
+            g, j = divmod(k, 4)
+            u_t, negm, rstd = st[k]
             z = work.tile([P, D], F32, tag="z", bufs=3)
-            if XHAT_ON_SCALAR:
-                nb = small.tile([P, 1], F32, tag="nb")
-                nc.vector.tensor_tensor(out=nb[:], in0=negm[:], in1=rstd[:], op=ALU.mult)
-                nc.scalar.activation(out=z[:], in_=u_t[:], func=ACT.Identity, bias=nb[:], scale=rstd[:])
-            else:
-                nc.vector.tensor_scalar(
-                    out=z[:], in0=u_t[:], scalar1=negm[:], scalar2=rstd[:], op0=ALU.add, op1=ALU.mult
-                )
-
+            nc.vector.tensor_scalar(out=z[:], in0=u_t[:], scalar1=negm[:], scalar2=rstd[:], op0=ALU.add, op1=ALU.mult)
             hp = work.tile([P, 8, P], BF16, tag="hp", bufs=3)
             for a in range(2):
                 zT = psum.tile([P, 4, P], F32, tag="zT", bufs=2)
                 for t in range(4):
                     c = 4 * a + t
                     nc.tensor.transpose(zT[:, t, :], z[:, P * c : P * c + P], ident_f[:])
-                bank = 2 * k + a
-                on_vector = AFFINE_ON_VECTOR_EVERY > 0 and bank % AFFINE_ON_VECTOR_EVERY == 0
                 for t in range(4):
                     c = 4 * a + t
-                    if on_vector:
-                        nc.vector.tensor_scalar(
-                            out=hp[:, c, :], in0=zT[:, t, :], scalar1=gb[:, c : c + 1],
-                            scalar2=gb[:, 8 + c : 9 + c], op0=ALU.mult, op1=ALU.add,
-                        )
-                    else:
-                        nc.scalar.activation(
-                            out=hp[:, c, :], in_=zT[:, t, :], func=ACT.Identity,
-                            bias=gb[:, 8 + c : 9 + c], scale=gb[:, c : c + 1],
-                        )
+                    nc.scalar.activation(
+                        out=hp[:, c, :], in_=zT[:, t, :], func=ACT.Identity,
+                        bias=gb[:, 8 + c : 9 + c], scale=gb[:, c : c + 1],
+                    )
             hg = work.tile([P, 2, P, 4], BF16, tag="hg", bufs=3, align_bytes=64)
-            nc.vector.tensor_copy(out=hg[:], in_=hp[:].rearrange("p (a t) b -> p a b t", t=4))
+            nc.vector.tensor_copy(
+                out=hg[:].rearrange("p a (c i) t -> p a c t i", i=4),
+                in_=hp[:].rearrange("p (a t) (c i) -> p a c t i", t=4, i=4),
+            )
             hc = work.tile([P, 2 * P], U32, tag="hc", bufs=3, align_bytes=64)
             hs = work.tile([P, 2 * P], U8, tag="hs", bufs=3, align_bytes=64)
             nc.vector.quantize_mx(out=hc[:].bitcast(FP8X4), scales=hs[:], in_=hg[:].rearrange("p a b t -> p (a b t)"))
 
             dg = work.tile([P, 2, G, 4], BF16, tag="dg", bufs=3, align_bytes=64)
-            nc.vector.tensor_copy(out=dg[:], in_=dup_t[k // 4][:, k % 4].rearrange("p (a t) g -> p a g t", t=4))
+            nc.vector.tensor_copy(
+                out=dg[:].rearrange("p a (c i) t -> p a c t i", i=4),
+                in_=dup_t[g][:, j].rearrange("p (a t) (c i) -> p a c t i", t=4, i=4),
+            )
             dc = work.tile([P, 2 * G], U32, tag="dc", bufs=3, align_bytes=64)
             ds = work.tile([P, 2 * G], U8, tag="ds", bufs=3, align_bytes=64)
             nc.vector.quantize_mx(out=dc[:].bitcast(FP8X4), scales=ds[:], in_=dg[:].rearrange("p a g t -> p (a g t)"))
 
-            if k % 4 == 0:
-                o2 = psum.tile([P, 4 * G], F32, tag="o2", bufs=1)
-                o2_t[k // 4] = o2
-            o2 = o2_t[k // 4]
+            if j == 0:
+                o2_new = psum.tile([P, 4 * G], F32, tag="o2", bufs=1)
+                o2_t[g] = o2_new
+            o2 = o2_t[g]
             for a in range(2):
                 sl = slice(P * a, P * a + P)
                 nc.tensor.matmul_mx(
-                    out=o2[:, G * (k % 4) : G * (k % 4) + G],
+                    out=o2[:, G * j : G * j + G],
                     lhsT=hc[:, sl].bitcast(FP8X4),
                     lhsT_scale=hs[:, sl],
                     rhs=dc[:, sl].bitcast(FP8X4),
@@ -207,8 +209,28 @@ def tile_mldecoder_pb_t_kernel(tc, ff_hid, tgt, w2, b2, g3, be3, dup_pool, dup_b
                     start=(a == 0),
                     stop=(a == 1),
                 )
-            if k % 4 == 3:
-                o_cols = slice(G * (k - 3), G * (k + 1))
+            if j == 3:
+                o_cols = slice(4 * G * g, 4 * G * g + 4 * G)
                 ob = work.tile([P, 4 * G], F32, tag="ob", bufs=3)
                 nc.vector.tensor_tensor(out=ob[:], in0=o2[:], in1=dbias[:, o_cols], op=ALU.add)
                 nc.sync.dma_start(out=out[:, o_cols], in_=ob[:])
+
+        ff_prep(0)
+        for c in range(8):
+            mx_chunk(0, c)
+        ff_prep(1)
+        for k in range(K + 1):
+            g, j = divmod(k, 4)
+            if k < K:
+                if j == 0 and g + 1 < NG:
+                    load_group(g + 1)
+                    if g % 2 == 0 and g // 2 + 1 < 4:
+                        load_ffh(g // 2 + 1)
+                front(k)
+                if g + 1 < NG:
+                    mx_chunk(g + 1, 2 * j)
+                    mx_chunk(g + 1, 2 * j + 1)
+                if j == 3 and g + 2 < NG:
+                    ff_prep(g + 2)
+            if k >= 1:
+                back(k - 1)

@@ -15,17 +15,60 @@ P = 128
 B, K, G, D, FF = 128, 32, 128, 1024, 512
 EPS = 1e-5
 FLOPS = 2 * B * K * FF * D + 2 * B * K * D * G
-NG = K // 4
 
 
 def tile_mldecoder_pb_t_kernel(tc, ff_hid, tgt, w2, b2, g3, be3, dup_pool, dup_bias, out):
     nc = tc.nc
     with ExitStack() as ctx:
         const = ctx.enter_context(tc.tile_pool(name="const", bufs=1))
-        loads = ctx.enter_context(tc.tile_pool(name="loads", bufs=3))
-        work = ctx.enter_context(tc.tile_pool(name="work", bufs=3))
-        small = ctx.enter_context(tc.tile_pool(name="small", bufs=6))
-        psum = ctx.enter_context(tc.psum_pool(name="psum", bufs=1))
+        loads = ctx.enter_context(tc.tile_pool(name="loads", bufs=5))
+        work = ctx.enter_context(tc.tile_pool(name="work", bufs=2))
+        small = ctx.enter_context(tc.tile_pool(name="small", bufs=8))
+        psum = ctx.enter_context(tc.psum_pool(name="psum", bufs=2))
+        ctx.enter_context(tc.manual_schedule())
+
+        ffh_t, tgt_t, dup_t = {}, {}, {}
+        ffT_t, ffg_t, ff_q = {}, {}, {}
+        u_of, s1_of, s0_of, negm_of, ss_of, rstd_of, nb_of = {}, {}, {}, {}, {}, {}, {}
+        z_of, zT_of, hp_of, hg_of, h_q, dg_of, d_q, o2_t = {}, {}, {}, {}, {}, {}, {}, {}
+
+        def load_ffh(r):
+            ffh = loads.tile([P, 4, FF], BF16, tag="ffh", bufs=3)
+            nc.sync.dma_start(out=ffh[:], in_=ff_hid[:, 4 * r : 4 * r + 4, :])
+            ffh_t[r] = ffh
+
+        def load_tgt(p):
+            tg = loads.tile([P, 2, D], BF16, tag="tg", bufs=5)
+            nc.sync.dma_start(out=tg[:], in_=tgt[:, 2 * p : 2 * p + 2, :])
+            tgt_t[p] = tg
+
+        def load_dup(p):
+            dr = loads.tile([P, 2, 8, G], BF16, tag="dr", bufs=5)
+            nc.sync.dma_start(out=dr[:], in_=dup_pool[2 * p : 2 * p + 2].rearrange("k (c p) g -> p k c g", p=P))
+            dup_t[p] = dr
+
+        w2raw = const.tile([P, 4, D], BF16)
+        for u in range(2):
+            nc.sync.dma_start(
+                out=w2raw[:, 2 * u : 2 * u + 2, :],
+                in_=w2[256 * u : 256 * u + 256, :].rearrange("(q e) c -> q e c", e=2),
+            )
+        load_ffh(0)
+        b2bc = const.tile([P, D], BF16)
+        nc.sync.dma_start(out=b2bc[:], in_=b2.partition_broadcast(P))
+        load_tgt(0)
+        gb_raw = const.tile([P, P], BF16)
+        nc.vector.memset(gb_raw[:], 0.0)
+        nc.sync.dma_start(out=gb_raw[0:8, :], in_=g3.rearrange("(c p) -> c p", p=P))
+        nc.sync.dma_start(out=gb_raw[8:16, :], in_=be3.rearrange("(c p) -> c p", p=P))
+        load_dup(0)
+        load_tgt(1)
+        load_dup(1)
+        load_ffh(1)
+        load_tgt(2)
+        load_dup(2)
+        dbias = const.tile([P, K * G], BF16)
+        nc.sync.dma_start(out=dbias[:], in_=dup_bias.partition_broadcast(P))
 
         mhalf = const.tile([P, 1], F32)
         nc.vector.memset(mhalf[:], -0.5)
@@ -34,174 +77,186 @@ def tile_mldecoder_pb_t_kernel(tc, ff_hid, tgt, w2, b2, g3, be3, dup_pool, dup_b
         ident_b = const.tile([P, P], BF16)
         make_identity(nc, ident_b[:])
 
-        w2raw = const.tile([P, 4, D], BF16)
-        for u in range(2):
-            nc.sync.dma_start(
-                out=w2raw[:, 2 * u : 2 * u + 2, :],
-                in_=w2[256 * u : 256 * u + 256, :].rearrange("(q e) c -> q e c", e=2),
-            )
-        gb_raw = const.tile([P, P], BF16)
-        nc.vector.memset(gb_raw[:], 0.0)
-        nc.sync.dma_start(out=gb_raw[0:8, :], in_=g3.rearrange("(c p) -> c p", p=P))
-        nc.sync.dma_start(out=gb_raw[8:16, :], in_=be3.rearrange("(c p) -> c p", p=P))
-        nc.sync.dma_start(out=gb_raw[16:24, :], in_=b2.rearrange("(c p) -> c p", p=P))
-
-        ffh_t = {}
-        tgt_t = {}
-        dup_t = {}
-
-        def load_ffh(i):
-            ffh = loads.tile([P, 8, FF], BF16, tag="ffh", bufs=4)
-            nc.sync.dma_start(out=ffh[:], in_=ff_hid[:, 8 * i : 8 * i + 8, :])
-            ffh_t[i] = ffh
-
-        def load_group(g):
-            tg = loads.tile([P, 4, D], BF16, tag="tg", bufs=3)
-            nc.sync.dma_start(out=tg[:], in_=tgt[:, 4 * g : 4 * g + 4, :])
-            tgt_t[g] = tg
-            dr = loads.tile([P, 4, 8, G], BF16, tag="dr", bufs=3)
-            nc.sync.dma_start(out=dr[:], in_=dup_pool[4 * g : 4 * g + 4].rearrange("k (c p) g -> p k c g", p=P))
-            dup_t[g] = dr
-
-        load_ffh(0)
-        load_group(0)
-        dbias = const.tile([P, K * G], BF16)
-        nc.sync.dma_start(out=dbias[:], in_=dup_bias.partition_broadcast(P))
-
         w2c = const.tile([P, D], U32, align_bytes=64)
         w2s = const.tile([P, D], U8, align_bytes=64)
         w2g = const.tile([P, 2, 512, 4], BF16, align_bytes=64)
-        for h in range(2):
-            nc.vector.tensor_copy(
-                out=w2g[:, h].rearrange("p (c i) t -> p c t i", i=4),
-                in_=w2raw[:, :, 512 * h : 512 * h + 512].rearrange("p t (c i) -> p c t i", i=4),
-            )
-        for h in range(2):
+        nc.vector.tensor_copy(
+            out=w2g[:, 0].rearrange("p (c i) t -> p c t i", i=4),
+            in_=w2raw[:, :, 0:512].rearrange("p t (c i) -> p c t i", i=4),
+        )
+        nc.scalar.copy(
+            out=w2g[:, 1].rearrange("p (c i) t -> p c t i", i=4),
+            in_=w2raw[:, :, 512:1024].rearrange("p t (c i) -> p c t i", i=4),
+        )
+
+        def quant_w2(h):
             nc.vector.quantize_mx(
                 out=w2c[:, 512 * h : 512 * h + 512].bitcast(FP8X4),
                 scales=w2s[:, 512 * h : 512 * h + 512],
                 in_=w2g[:, h].rearrange("p c t -> p (c t)"),
             )
 
-        gb_ps = psum.tile([P, P], BF16, tag="ffhT", bufs=1)
-        nc.tensor.transpose(gb_ps[:], gb_raw[:], ident_b[:])
-        gb = const.tile([P, 24], F32)
-        nc.vector.tensor_copy(out=gb[:], in_=gb_ps[:, 0:24])
+        gb = const.tile([P, 16], F32)
 
-        ff_q = {}
-        ffb_t = {}
-        o2_t = {}
-        st = {}
+        def gain_shift_columns():
+            gb_ps = psum.tile([P, P], BF16, tag="o2", bufs=2)
+            nc.tensor.transpose(gb_ps[:], gb_raw[:], ident_b[:])
+            nc.vector.tensor_copy(out=gb[:], in_=gb_ps[:, 0:16])
 
-        def ff_prep(g):
-            ffc = work.tile([P, 4 * P], U32, tag="ffc", bufs=2, align_bytes=64)
-            ffs = work.tile([P, 4 * P], U8, tag="ffs", bufs=2, align_bytes=64)
-            for pair in range(2):
-                ffhT = psum.tile([P, 2, 2, P], F32, tag="ffhT", bufs=1)
-                for j in range(2):
-                    k = 4 * g + 2 * pair + j
-                    words = ffh_t[k // 8][:, k % 8, :].bitcast(F32)
-                    for u in range(2):
-                        nc.tensor.transpose(ffhT[:, j, u, :], words[:, P * u : P * u + P], ident_f[:])
-                ffg = work.tile([P, 2, P, 4], BF16, tag="ffg", bufs=2, align_bytes=64)
-                nc.scalar.copy(out=ffg[:].bitcast(F32), in_=ffhT[:].rearrange("p j u b -> p j b u"))
-                sl = slice(2 * P * pair, 2 * P * pair + 2 * P)
-                nc.vector.quantize_mx(
-                    out=ffc[:, sl].bitcast(FP8X4), scales=ffs[:, sl], in_=ffg[:].rearrange("p j b t -> p (j b t)")
-                )
-            ff_q[g] = (ffc, ffs)
+        def t_ff(p):
+            ffT = psum.tile([P, 2, 2, P], F32, tag="ffT", bufs=1)
+            for j in range(2):
+                k = 2 * p + j
+                words = ffh_t[k // 4][:, k % 4, :].bitcast(F32)
+                for u in range(2):
+                    nc.tensor.transpose(ffT[:, j, u, :], words[:, P * u : P * u + P], ident_f[:])
+            ffT_t[p] = ffT
 
-        def mx_chunk(g, c):
-            ffc, ffs = ff_q[g]
-            mm = psum.tile([P, 4 * P], F32, tag="mm", bufs=2)
-            sl = slice(P * c, P * c + P)
-            nc.tensor.matmul_mx(
-                out=mm[:],
-                lhsT=w2c[:, sl].bitcast(FP8X4),
-                lhsT_scale=w2s[:, sl],
-                rhs=ffc[:].bitcast(FP8X4),
-                rhs_scale=ffs[:],
-                start=True,
-                stop=True,
+        def c_ff(p):
+            ffg = work.tile([P, 2, P, 4], BF16, tag="ffg", bufs=2, align_bytes=64)
+            nc.scalar.copy(out=ffg[:].bitcast(F32), in_=ffT_t[p][:].rearrange("p j u b -> p j b u"))
+            ffg_t[p] = ffg
+
+        def q_ff(p):
+            ffc = work.tile([P, 2 * P], U32, tag="ffc", bufs=3, align_bytes=64)
+            ffs = work.tile([P, 2 * P], U8, tag="ffs", bufs=3, align_bytes=64)
+            nc.vector.quantize_mx(
+                out=ffc[:].bitcast(FP8X4), scales=ffs[:], in_=ffg_t[p][:].rearrange("p j b t -> p (j b t)")
             )
-            ffb = work.tile([P, 4 * P], F32, tag="ffb", bufs=16)
-            nc.scalar.activation(out=ffb[:], in_=mm[:], func=ACT.Identity, bias=gb[:, 16 + c : 17 + c], scale=1.0)
-            ffb_t[(g, c)] = ffb
+            ff_q[p] = (ffc, ffs)
 
-        def front(k):
-            g, j = divmod(k, 4)
-            u_t = work.tile([P, D], F32, tag="u", bufs=4)
+        def tb(k):
+            u_t = work.tile([P, D], F32, tag="u", bufs=7)
+            nc.vector.tensor_tensor(out=u_t[:], in0=tgt_t[k // 2][:, k % 2, :], in1=b2bc[:], op=ALU.add)
+            u_of[k] = u_t
+
+        def m1(k):
+            ffc, ffs = ff_q[k // 2]
+            cols = slice(P * (k % 2), P * (k % 2) + P)
+            banks = []
+            for h in range(2):
+                s1 = psum.tile([P, 512], F32, tag="s1", bufs=2)
+                n_cols = slice(512 * h, 512 * h + 512)
+                nc.tensor.matmul_mx(
+                    out=s1[:],
+                    lhsT=ffc[:, cols].bitcast(FP8X4),
+                    lhsT_scale=ffs[:, cols],
+                    rhs=w2c[:, n_cols].bitcast(FP8X4),
+                    rhs_scale=w2s[:, n_cols],
+                    start=True,
+                    stop=True,
+                )
+                banks.append(s1)
+            s1_of[k] = banks
+
+        def p1(k):
             s0 = small.tile([P, 2], F32, tag="s0")
             for h in range(2):
-                s1 = psum.tile([P, 4, P], F32, tag="s1", bufs=2)
-                for t in range(4):
-                    nc.tensor.transpose(s1[:, t, :], ffb_t[(g, 4 * h + t)][:, P * j : P * j + P], ident_f[:])
                 n_cols = slice(512 * h, 512 * h + 512)
                 nc.vector.scalar_tensor_tensor(
-                    out=u_t[:, n_cols],
-                    in0=s1[:].rearrange("p t d -> p (t d)"),
-                    scalar=1.0,
-                    in1=tgt_t[g][:, j, n_cols],
-                    op0=ALU.mult,
-                    op1=ALU.add,
-                    accum_out=s0[:, h : h + 1],
+                    out=u_of[k][:, n_cols], in0=s1_of[k][h][:], scalar=1.0, in1=u_of[k][:, n_cols],
+                    op0=ALU.mult, op1=ALU.add, accum_out=s0[:, h : h + 1],
                 )
+            s0_of[k] = s0
+
+        def nm(k):
             negm = small.tile([P, 1], F32, tag="negm")
+            s0 = s0_of[k]
             nc.gpsimd.tensor_scalar(
                 out=negm[:], in0=s0[:, 0:1], scalar1=s0[:, 1:2], scalar2=-1.0 / D, op0=ALU.add, op1=ALU.mult
             )
-            junk = work.tile([P, D], BF16, tag="junk", bufs=2)
+            negm_of[k] = negm
+
+        def sq(k):
+            junk = work.tile([P, D], BF16, tag="junk", bufs=1)
             ss = small.tile([P, 1], F32, tag="ss")
-            nc.scalar.activation(out=junk[:], in_=u_t[:], func=ACT.Square, bias=negm[:], scale=1.0, accum_out=ss[:])
+            nc.scalar.activation(
+                out=junk[:], in_=u_of[k][:], func=ACT.Square, bias=negm_of[k][:], scale=1.0, accum_out=ss[:]
+            )
+            ss_of[k] = ss
+
+        def rs(k):
             ve = small.tile([P, 1], F32, tag="ve")
-            nc.gpsimd.tensor_scalar(out=ve[:], in0=ss[:], scalar1=1.0 / D, scalar2=EPS, op0=ALU.mult, op1=ALU.add)
+            nc.gpsimd.tensor_scalar(
+                out=ve[:], in0=ss_of[k][:], scalar1=1.0 / D, scalar2=EPS, op0=ALU.mult, op1=ALU.add
+            )
             rstd = small.tile([P, 1], F32, tag="rstd")
             nc.gpsimd.tensor_tensor(out=rstd[:], in0=ve[:], in1=mhalf[:], op=ALU.pow)
-            st[k] = (u_t, negm, rstd)
+            nb = small.tile([P, 1], F32, tag="nb")
+            nc.gpsimd.tensor_tensor(out=nb[:], in0=negm_of[k][:], in1=rstd[:], op=ALU.mult)
+            rstd_of[k] = rstd
+            nb_of[k] = nb
 
-        def back(k):
-            g, j = divmod(k, 4)
-            u_t, negm, rstd = st[k]
-            z = work.tile([P, D], F32, tag="z", bufs=3)
-            nc.vector.tensor_scalar(out=z[:], in0=u_t[:], scalar1=negm[:], scalar2=rstd[:], op0=ALU.add, op1=ALU.mult)
-            hp = work.tile([P, 8, P], BF16, tag="hp", bufs=3)
+        def xh(k):
+            z = work.tile([P, D], F32, tag="z", bufs=2)
+            nc.scalar.activation(
+                out=z[:], in_=u_of[k][:], func=ACT.Identity, bias=nb_of[k][:], scale=rstd_of[k][:]
+            )
+            z_of[k] = z
+
+        def tz(k):
+            banks = []
             for a in range(2):
                 zT = psum.tile([P, 4, P], F32, tag="zT", bufs=2)
                 for t in range(4):
                     c = 4 * a + t
-                    nc.tensor.transpose(zT[:, t, :], z[:, P * c : P * c + P], ident_f[:])
+                    nc.tensor.transpose(zT[:, t, :], z_of[k][:, P * c : P * c + P], ident_f[:])
+                banks.append(zT)
+            zT_of[k] = banks
+
+        def af(k):
+            hp = work.tile([P, 8, P], BF16, tag="hp", bufs=2)
+            for a in range(2):
                 for t in range(4):
                     c = 4 * a + t
                     nc.scalar.activation(
-                        out=hp[:, c, :], in_=zT[:, t, :], func=ACT.Identity,
+                        out=hp[:, c, :], in_=zT_of[k][a][:, t, :], func=ACT.Identity,
                         bias=gb[:, 8 + c : 9 + c], scale=gb[:, c : c + 1],
                     )
-            hg = work.tile([P, 2, P, 4], BF16, tag="hg", bufs=3, align_bytes=64)
+            hp_of[k] = hp
+
+        def rg(k):
+            hg = work.tile([P, 2, P, 4], BF16, tag="hg", bufs=2, align_bytes=64)
             nc.vector.tensor_copy(
                 out=hg[:].rearrange("p a (c i) t -> p a c t i", i=4),
-                in_=hp[:].rearrange("p (a t) (c i) -> p a c t i", t=4, i=4),
+                in_=hp_of[k][:].rearrange("p (a t) (c i) -> p a c t i", t=4, i=4),
             )
+            hg_of[k] = hg
+
+        def qh(k):
             hc = work.tile([P, 2 * P], U32, tag="hc", bufs=3, align_bytes=64)
             hs = work.tile([P, 2 * P], U8, tag="hs", bufs=3, align_bytes=64)
-            nc.vector.quantize_mx(out=hc[:].bitcast(FP8X4), scales=hs[:], in_=hg[:].rearrange("p a b t -> p (a b t)"))
+            nc.vector.quantize_mx(
+                out=hc[:].bitcast(FP8X4), scales=hs[:], in_=hg_of[k][:].rearrange("p a b t -> p (a b t)")
+            )
+            h_q[k] = (hc, hs)
 
+        def dr(k):
             dg = work.tile([P, 2, G, 4], BF16, tag="dg", bufs=3, align_bytes=64)
             nc.vector.tensor_copy(
                 out=dg[:].rearrange("p a (c i) t -> p a c t i", i=4),
-                in_=dup_t[g][:, j].rearrange("p (a t) (c i) -> p a c t i", t=4, i=4),
+                in_=dup_t[k // 2][:, k % 2].rearrange("p (a t) (c i) -> p a c t i", t=4, i=4),
             )
-            dc = work.tile([P, 2 * G], U32, tag="dc", bufs=3, align_bytes=64)
-            ds = work.tile([P, 2 * G], U8, tag="ds", bufs=3, align_bytes=64)
-            nc.vector.quantize_mx(out=dc[:].bitcast(FP8X4), scales=ds[:], in_=dg[:].rearrange("p a g t -> p (a g t)"))
+            dg_of[k] = dg
 
-            if j == 0:
-                o2_new = psum.tile([P, 4 * G], F32, tag="o2", bufs=1)
-                o2_t[g] = o2_new
-            o2 = o2_t[g]
+        def qd(k):
+            dc = work.tile([P, 2 * G], U32, tag="dc", bufs=9, align_bytes=64)
+            ds = work.tile([P, 2 * G], U8, tag="ds", bufs=9, align_bytes=64)
+            nc.vector.quantize_mx(
+                out=dc[:].bitcast(FP8X4), scales=ds[:], in_=dg_of[k][:].rearrange("p a g t -> p (a g t)")
+            )
+            d_q[k] = (dc, ds)
+
+        def m2(k):
+            if k % 4 == 0:
+                o2_new = psum.tile([P, 4 * G], F32, tag="o2", bufs=2)
+                o2_t[k // 4] = o2_new
+            hc, hs = h_q[k]
+            dc, ds = d_q[k]
             for a in range(2):
                 sl = slice(P * a, P * a + P)
                 nc.tensor.matmul_mx(
-                    out=o2[:, G * j : G * j + G],
+                    out=o2_t[k // 4][:, G * (k % 4) : G * (k % 4) + G],
                     lhsT=hc[:, sl].bitcast(FP8X4),
                     lhsT_scale=hs[:, sl],
                     rhs=dc[:, sl].bitcast(FP8X4),
@@ -209,28 +264,63 @@ def tile_mldecoder_pb_t_kernel(tc, ff_hid, tgt, w2, b2, g3, be3, dup_pool, dup_b
                     start=(a == 0),
                     stop=(a == 1),
                 )
-            if j == 3:
-                o_cols = slice(4 * G * g, 4 * G * g + 4 * G)
-                ob = work.tile([P, 4 * G], F32, tag="ob", bufs=3)
-                nc.vector.tensor_tensor(out=ob[:], in0=o2[:], in1=dbias[:, o_cols], op=ALU.add)
-                nc.sync.dma_start(out=out[:, o_cols], in_=ob[:])
 
-        ff_prep(0)
-        for c in range(8):
-            mx_chunk(0, c)
-        ff_prep(1)
-        for k in range(K + 1):
-            g, j = divmod(k, 4)
-            if k < K:
-                if j == 0 and g + 1 < NG:
-                    load_group(g + 1)
-                    if g % 2 == 0 and g // 2 + 1 < 4:
-                        load_ffh(g // 2 + 1)
-                front(k)
-                if g + 1 < NG:
-                    mx_chunk(g + 1, 2 * j)
-                    mx_chunk(g + 1, 2 * j + 1)
-                if j == 3 and g + 2 < NG:
-                    ff_prep(g + 2)
-            if k >= 1:
-                back(k - 1)
+        def oa(g):
+            o_cols = slice(4 * G * g, 4 * G * g + 4 * G)
+            ob = work.tile([P, 4 * G], F32, tag="ob", bufs=2)
+            nc.vector.tensor_tensor(out=ob[:], in0=o2_t[g][:], in1=dbias[:, o_cols], op=ALU.add)
+            nc.sync.dma_start(out=out[:, o_cols], in_=ob[:])
+
+        def tok(k):
+            return 0 <= k < K
+
+        for n in range(-4, K + 6):
+            if n % 2 == 0:
+                p_new = (n + 8) // 2
+                if 3 <= p_new < K // 2:
+                    load_tgt(p_new)
+                    load_dup(p_new)
+            if (n + 10) % 4 == 0:
+                r_new = (n + 10) // 4
+                if 2 <= r_new < K // 4:
+                    load_ffh(r_new)
+            if tok(n):
+                p1(n)
+                nm(n)
+            if tok(n - 4):
+                af(n - 4)
+            if n == -4:
+                quant_w2(0)
+            if tok(n + 2):
+                tb(n + 2)
+            if n == -4:
+                quant_w2(1)
+            if tok(n + 1):
+                m1(n + 1)
+            if tok(n - 4):
+                rg(n - 4)
+            if tok(n - 3):
+                xh(n - 3)
+            if tok(n - 5):
+                m2(n - 5)
+            if tok(n + 2):
+                dr(n + 2)
+            if tok(n - 3):
+                tz(n - 3)
+            if tok(n - 1):
+                sq(n - 1)
+                rs(n - 1)
+            if tok(n - 4):
+                qh(n - 4)
+            if tok(n + 1):
+                qd(n + 1)
+            if (n + 4) % 2 == 0 and tok(n + 4):
+                t_ff((n + 4) // 2)
+            if (n + 3) % 2 == 0 and tok(n + 3):
+                c_ff((n + 3) // 2)
+            if (n + 2) % 2 == 0 and tok(n + 2):
+                q_ff((n + 2) // 2)
+            if n == -1:
+                gain_shift_columns()
+            if tok(n - 5) and (n - 5) % 4 == 3:
+                oa((n - 5) // 4)

@@ -15,6 +15,7 @@ P = 128
 B, K, G, D, FF = 128, 32, 128, 1024, 512
 EPS = 1e-5
 FLOPS = 2 * B * K * FF * D + 2 * B * K * D * G
+DUP_ON_GPSIMD = True
 
 
 def tile_mldecoder_pb_t_kernel(tc, ff_hid, tgt, w2, b2, g3, be3, dup_pool, dup_bias, out):
@@ -23,19 +24,19 @@ def tile_mldecoder_pb_t_kernel(tc, ff_hid, tgt, w2, b2, g3, be3, dup_pool, dup_b
         const = ctx.enter_context(tc.tile_pool(name="const", bufs=1))
         loads = ctx.enter_context(tc.tile_pool(name="loads", bufs=5))
         work = ctx.enter_context(tc.tile_pool(name="work", bufs=2))
-        small = ctx.enter_context(tc.tile_pool(name="small", bufs=8))
+        small = ctx.enter_context(tc.tile_pool(name="small", bufs=6))
         psum = ctx.enter_context(tc.psum_pool(name="psum", bufs=2))
         ctx.enter_context(tc.manual_schedule())
 
         ffh_t, tgt_t, dup_t = {}, {}, {}
         ffT_t, ffg_t, ff_q = {}, {}, {}
-        u_of, s1_of, s0_of, negm_of, ss_of, rstd_of, nb_of = {}, {}, {}, {}, {}, {}, {}
+        u_of, s1_of, s0_of, negm_of, ss_of, std_of, rstd_of, nb_of = {}, {}, {}, {}, {}, {}, {}, {}
         z_of, zT_of, hp_of, hg_of, h_q, dg_of, d_q, o2_t = {}, {}, {}, {}, {}, {}, {}, {}
 
-        def load_ffh(r):
-            ffh = loads.tile([P, 4, FF], BF16, tag="ffh", bufs=3)
-            nc.sync.dma_start(out=ffh[:], in_=ff_hid[:, 4 * r : 4 * r + 4, :])
-            ffh_t[r] = ffh
+        def load_ffh(p):
+            ffh = loads.tile([P, 2, FF], BF16, tag="ffh", bufs=4)
+            nc.sync.dma_start(out=ffh[:], in_=ff_hid[:, 2 * p : 2 * p + 2, :])
+            ffh_t[p] = ffh
 
         def load_tgt(p):
             tg = loads.tile([P, 2, D], BF16, tag="tg", bufs=5)
@@ -43,35 +44,38 @@ def tile_mldecoder_pb_t_kernel(tc, ff_hid, tgt, w2, b2, g3, be3, dup_pool, dup_b
             tgt_t[p] = tg
 
         def load_dup(p):
-            dr = loads.tile([P, 2, 8, G], BF16, tag="dr", bufs=5)
-            nc.sync.dma_start(out=dr[:], in_=dup_pool[2 * p : 2 * p + 2].rearrange("k (c p) g -> p k c g", p=P))
-            dup_t[p] = dr
+            dr_t = loads.tile([P, 2, 8, G], BF16, tag="dr", bufs=5)
+            nc.sync.dma_start(out=dr_t[:], in_=dup_pool[2 * p : 2 * p + 2].rearrange("k (c p) g -> p k c g", p=P))
+            dup_t[p] = dr_t
 
+        load_ffh(0)
         w2raw = const.tile([P, 4, D], BF16)
         for u in range(2):
             nc.sync.dma_start(
                 out=w2raw[:, 2 * u : 2 * u + 2, :],
                 in_=w2[256 * u : 256 * u + 256, :].rearrange("(q e) c -> q e c", e=2),
             )
-        load_ffh(0)
         b2bc = const.tile([P, D], BF16)
         nc.sync.dma_start(out=b2bc[:], in_=b2.partition_broadcast(P))
         load_tgt(0)
+        load_dup(0)
         gb_raw = const.tile([P, P], BF16)
         nc.vector.memset(gb_raw[:], 0.0)
         nc.sync.dma_start(out=gb_raw[0:8, :], in_=g3.rearrange("(c p) -> c p", p=P))
         nc.sync.dma_start(out=gb_raw[8:16, :], in_=be3.rearrange("(c p) -> c p", p=P))
-        load_dup(0)
+        load_ffh(1)
         load_tgt(1)
         load_dup(1)
-        load_ffh(1)
+        load_ffh(2)
         load_tgt(2)
         load_dup(2)
         dbias = const.tile([P, K * G], BF16)
         nc.sync.dma_start(out=dbias[:], in_=dup_bias.partition_broadcast(P))
 
-        mhalf = const.tile([P, 1], F32)
-        nc.vector.memset(mhalf[:], -0.5)
+        eps_t = const.tile([P, 1], F32)
+        nc.vector.memset(eps_t[:], EPS)
+        warm = const.tile([P, 1], F32)
+        nc.scalar.activation(out=warm[:], in_=eps_t[:], func=ACT.Sqrt)
         ident_f = const.tile([P, P], F32)
         make_identity(nc, ident_f[:])
         ident_b = const.tile([P, P], BF16)
@@ -107,7 +111,7 @@ def tile_mldecoder_pb_t_kernel(tc, ff_hid, tgt, w2, b2, g3, be3, dup_pool, dup_b
             ffT = psum.tile([P, 2, 2, P], F32, tag="ffT", bufs=1)
             for j in range(2):
                 k = 2 * p + j
-                words = ffh_t[k // 4][:, k % 4, :].bitcast(F32)
+                words = ffh_t[p][:, j, :].bitcast(F32)
                 for u in range(2):
                     nc.tensor.transpose(ffT[:, j, u, :], words[:, P * u : P * u + P], ident_f[:])
             ffT_t[p] = ffT
@@ -126,7 +130,7 @@ def tile_mldecoder_pb_t_kernel(tc, ff_hid, tgt, w2, b2, g3, be3, dup_pool, dup_b
             ff_q[p] = (ffc, ffs)
 
         def tb(k):
-            u_t = work.tile([P, D], F32, tag="u", bufs=7)
+            u_t = work.tile([P, D], F32, tag="u", bufs=6)
             nc.vector.tensor_tensor(out=u_t[:], in0=tgt_t[k // 2][:, k % 2, :], in1=b2bc[:], op=ALU.add)
             u_of[k] = u_t
 
@@ -135,7 +139,7 @@ def tile_mldecoder_pb_t_kernel(tc, ff_hid, tgt, w2, b2, g3, be3, dup_pool, dup_b
             cols = slice(P * (k % 2), P * (k % 2) + P)
             banks = []
             for h in range(2):
-                s1 = psum.tile([P, 512], F32, tag="s1", bufs=2)
+                s1 = psum.tile([P, 512], F32, tag="s1", bufs=3)
                 n_cols = slice(512 * h, 512 * h + 512)
                 nc.tensor.matmul_mx(
                     out=s1[:],
@@ -162,7 +166,7 @@ def tile_mldecoder_pb_t_kernel(tc, ff_hid, tgt, w2, b2, g3, be3, dup_pool, dup_b
         def nm(k):
             negm = small.tile([P, 1], F32, tag="negm")
             s0 = s0_of[k]
-            nc.gpsimd.tensor_scalar(
+            nc.vector.tensor_scalar(
                 out=negm[:], in0=s0[:, 0:1], scalar1=s0[:, 1:2], scalar2=-1.0 / D, op0=ALU.add, op1=ALU.mult
             )
             negm_of[k] = negm
@@ -173,18 +177,18 @@ def tile_mldecoder_pb_t_kernel(tc, ff_hid, tgt, w2, b2, g3, be3, dup_pool, dup_b
             nc.scalar.activation(
                 out=junk[:], in_=u_of[k][:], func=ACT.Square, bias=negm_of[k][:], scale=1.0, accum_out=ss[:]
             )
-            ss_of[k] = ss
+            std = small.tile([P, 1], F32, tag="std")
+            nc.scalar.activation(out=std[:], in_=ss[:], func=ACT.Sqrt, bias=eps_t[:], scale=1.0 / D)
+            std_of[k] = std
 
-        def rs(k):
-            ve = small.tile([P, 1], F32, tag="ve")
-            nc.gpsimd.tensor_scalar(
-                out=ve[:], in0=ss_of[k][:], scalar1=1.0 / D, scalar2=EPS, op0=ALU.mult, op1=ALU.add
-            )
+        def rc(k):
             rstd = small.tile([P, 1], F32, tag="rstd")
-            nc.gpsimd.tensor_tensor(out=rstd[:], in0=ve[:], in1=mhalf[:], op=ALU.pow)
-            nb = small.tile([P, 1], F32, tag="nb")
-            nc.gpsimd.tensor_tensor(out=nb[:], in0=negm_of[k][:], in1=rstd[:], op=ALU.mult)
+            nc.vector.reciprocal(out=rstd[:], in_=std_of[k][:])
             rstd_of[k] = rstd
+
+        def nbias(k):
+            nb = small.tile([P, 1], F32, tag="nb")
+            nc.scalar.activation(out=nb[:], in_=negm_of[k][:], func=ACT.Copy, scale=rstd_of[k][:])
             nb_of[k] = nb
 
         def xh(k):
@@ -216,7 +220,7 @@ def tile_mldecoder_pb_t_kernel(tc, ff_hid, tgt, w2, b2, g3, be3, dup_pool, dup_b
             hp_of[k] = hp
 
         def rg(k):
-            hg = work.tile([P, 2, P, 4], BF16, tag="hg", bufs=2, align_bytes=64)
+            hg = work.tile([P, 2, P, 4], BF16, tag="hg", bufs=3, align_bytes=64)
             nc.vector.tensor_copy(
                 out=hg[:].rearrange("p a (c i) t -> p a c t i", i=4),
                 in_=hp_of[k][:].rearrange("p (a t) (c i) -> p a c t i", t=4, i=4),
@@ -232,16 +236,22 @@ def tile_mldecoder_pb_t_kernel(tc, ff_hid, tgt, w2, b2, g3, be3, dup_pool, dup_b
             h_q[k] = (hc, hs)
 
         def dr(k):
-            dg = work.tile([P, 2, G, 4], BF16, tag="dg", bufs=3, align_bytes=64)
-            nc.vector.tensor_copy(
-                out=dg[:].rearrange("p a (c i) t -> p a c t i", i=4),
-                in_=dup_t[k // 2][:, k % 2].rearrange("p (a t) (c i) -> p a c t i", t=4, i=4),
-            )
+            dg = work.tile([P, 2, G, 4], BF16, tag="dg", bufs=2, align_bytes=64)
+            if DUP_ON_GPSIMD:
+                nc.gpsimd.tensor_scalar(
+                    out=dg[:], in0=dup_t[k // 2][:, k % 2].rearrange("p (a t) g -> p a g t", t=4),
+                    scalar1=1.0, scalar2=0.0, op0=ALU.mult, op1=ALU.add,
+                )
+            else:
+                nc.vector.tensor_copy(
+                    out=dg[:].rearrange("p a (c i) t -> p a c t i", i=4),
+                    in_=dup_t[k // 2][:, k % 2].rearrange("p (a t) (c i) -> p a c t i", t=4, i=4),
+                )
             dg_of[k] = dg
 
         def qd(k):
-            dc = work.tile([P, 2 * G], U32, tag="dc", bufs=9, align_bytes=64)
-            ds = work.tile([P, 2 * G], U8, tag="ds", bufs=9, align_bytes=64)
+            dc = work.tile([P, 2 * G], U32, tag="dc", bufs=8, align_bytes=64)
+            ds = work.tile([P, 2 * G], U8, tag="ds", bufs=8, align_bytes=64)
             nc.vector.quantize_mx(
                 out=dc[:].bitcast(FP8X4), scales=ds[:], in_=dg_of[k][:].rearrange("p a g t -> p (a g t)")
             )
@@ -274,53 +284,52 @@ def tile_mldecoder_pb_t_kernel(tc, ff_hid, tgt, w2, b2, g3, be3, dup_pool, dup_b
         def tok(k):
             return 0 <= k < K
 
-        for n in range(-4, K + 6):
+        for n in range(-4, K + 7):
             if n % 2 == 0:
                 p_new = (n + 8) // 2
                 if 3 <= p_new < K // 2:
+                    load_ffh(p_new)
                     load_tgt(p_new)
                     load_dup(p_new)
-            if (n + 10) % 4 == 0:
-                r_new = (n + 10) // 4
-                if 2 <= r_new < K // 4:
-                    load_ffh(r_new)
             if tok(n):
                 p1(n)
                 nm(n)
-            if tok(n - 4):
-                af(n - 4)
-            if n == -4:
-                quant_w2(0)
-            if tok(n + 2):
-                tb(n + 2)
-            if n == -4:
-                quant_w2(1)
+            if tok(n - 1):
+                rc(n - 1)
+            if tok(n - 6) and (n - 6) % 4 == 3:
+                oa((n - 6) // 4)
+            if tok(n - 2):
+                xh(n - 2)
             if tok(n + 1):
                 m1(n + 1)
-            if tok(n - 4):
-                rg(n - 4)
-            if tok(n - 3):
-                xh(n - 3)
             if tok(n - 5):
                 m2(n - 5)
-            if tok(n + 2):
-                dr(n + 2)
             if tok(n - 3):
-                tz(n - 3)
-            if tok(n - 1):
-                sq(n - 1)
-                rs(n - 1)
+                af(n - 3)
+            if n == -4:
+                quant_w2(0)
+                quant_w2(1)
+            if tok(n + 2):
+                tb(n + 2)
+            if tok(n - 2):
+                tz(n - 2)
+            if (n + 2) % 2 == 0 and tok(n + 2):
+                q_ff((n + 2) // 2)
             if tok(n - 4):
                 qh(n - 4)
+            if tok(n - 3):
+                rg(n - 3)
+            if tok(n):
+                sq(n)
+            if tok(n - 1):
+                nbias(n - 1)
             if tok(n + 1):
                 qd(n + 1)
+            if tok(n + 3):
+                dr(n + 3)
             if (n + 4) % 2 == 0 and tok(n + 4):
                 t_ff((n + 4) // 2)
             if (n + 3) % 2 == 0 and tok(n + 3):
                 c_ff((n + 3) // 2)
-            if (n + 2) % 2 == 0 and tok(n + 2):
-                q_ff((n + 2) // 2)
             if n == -1:
                 gain_shift_columns()
-            if tok(n - 5) and (n - 5) % 4 == 3:
-                oa((n - 5) // 4)

@@ -16,6 +16,8 @@ B, K, G, D, FF = 128, 32, 128, 1024, 512
 EPS = 1e-5
 FLOPS = 2 * B * K * FF * D + 2 * B * K * D * G
 DUP_ON_GPSIMD = True
+XH_ON_VECTOR_FROM = K
+AF_ON_VECTOR_EVERY = 4
 
 
 def tile_mldecoder_pb_t_kernel(tc, ff_hid, tgt, w2, b2, g3, be3, dup_pool, dup_bias, out):
@@ -48,6 +50,10 @@ def tile_mldecoder_pb_t_kernel(tc, ff_hid, tgt, w2, b2, g3, be3, dup_pool, dup_b
             nc.sync.dma_start(out=dr_t[:], in_=dup_pool[2 * p : 2 * p + 2].rearrange("k (c p) g -> p k c g", p=P))
             dup_t[p] = dr_t
 
+        gb_raw = const.tile([P, P], BF16)
+        nc.vector.memset(gb_raw[:], 0.0)
+        nc.sync.dma_start(out=gb_raw[0:8, :], in_=g3.rearrange("(c p) -> c p", p=P))
+        nc.sync.dma_start(out=gb_raw[8:16, :], in_=be3.rearrange("(c p) -> c p", p=P))
         load_ffh(0)
         w2raw = const.tile([P, 4, D], BF16)
         for u in range(2):
@@ -58,19 +64,14 @@ def tile_mldecoder_pb_t_kernel(tc, ff_hid, tgt, w2, b2, g3, be3, dup_pool, dup_b
         b2bc = const.tile([P, D], BF16)
         nc.sync.dma_start(out=b2bc[:], in_=b2.partition_broadcast(P))
         load_tgt(0)
-        load_dup(0)
-        gb_raw = const.tile([P, P], BF16)
-        nc.vector.memset(gb_raw[:], 0.0)
-        nc.sync.dma_start(out=gb_raw[0:8, :], in_=g3.rearrange("(c p) -> c p", p=P))
-        nc.sync.dma_start(out=gb_raw[8:16, :], in_=be3.rearrange("(c p) -> c p", p=P))
         load_ffh(1)
         load_tgt(1)
+        load_dup(0)
         load_dup(1)
         load_ffh(2)
         load_tgt(2)
         load_dup(2)
         dbias = const.tile([P, K * G], BF16)
-        nc.sync.dma_start(out=dbias[:], in_=dup_bias.partition_broadcast(P))
 
         eps_t = const.tile([P, 1], F32)
         nc.vector.memset(eps_t[:], EPS)
@@ -84,14 +85,16 @@ def tile_mldecoder_pb_t_kernel(tc, ff_hid, tgt, w2, b2, g3, be3, dup_pool, dup_b
         w2c = const.tile([P, D], U32, align_bytes=64)
         w2s = const.tile([P, D], U8, align_bytes=64)
         w2g = const.tile([P, 2, 512, 4], BF16, align_bytes=64)
-        nc.vector.tensor_copy(
-            out=w2g[:, 0].rearrange("p (c i) t -> p c t i", i=4),
-            in_=w2raw[:, :, 0:512].rearrange("p t (c i) -> p c t i", i=4),
-        )
-        nc.scalar.copy(
-            out=w2g[:, 1].rearrange("p (c i) t -> p c t i", i=4),
-            in_=w2raw[:, :, 512:1024].rearrange("p t (c i) -> p c t i", i=4),
-        )
+
+        def regroup_w2():
+            nc.vector.tensor_copy(
+                out=w2g[:, 0].rearrange("p (c i) t -> p c t i", i=4),
+                in_=w2raw[:, :, 0:512].rearrange("p t (c i) -> p c t i", i=4),
+            )
+            nc.scalar.copy(
+                out=w2g[:, 1].rearrange("p (c i) t -> p c t i", i=4),
+                in_=w2raw[:, :, 512:1024].rearrange("p t (c i) -> p c t i", i=4),
+            )
 
         def quant_w2(h):
             nc.vector.quantize_mx(
@@ -193,9 +196,14 @@ def tile_mldecoder_pb_t_kernel(tc, ff_hid, tgt, w2, b2, g3, be3, dup_pool, dup_b
 
         def xh(k):
             z = work.tile([P, D], F32, tag="z", bufs=2)
-            nc.scalar.activation(
-                out=z[:], in_=u_of[k][:], func=ACT.Identity, bias=nb_of[k][:], scale=rstd_of[k][:]
-            )
+            if k >= XH_ON_VECTOR_FROM:
+                nc.vector.tensor_scalar(
+                    out=z[:], in0=u_of[k][:], scalar1=negm_of[k][:], scalar2=rstd_of[k][:], op0=ALU.add, op1=ALU.mult
+                )
+            else:
+                nc.scalar.activation(
+                    out=z[:], in_=u_of[k][:], func=ACT.Identity, bias=nb_of[k][:], scale=rstd_of[k][:]
+                )
             z_of[k] = z
 
         def tz(k):
@@ -213,10 +221,16 @@ def tile_mldecoder_pb_t_kernel(tc, ff_hid, tgt, w2, b2, g3, be3, dup_pool, dup_b
             for a in range(2):
                 for t in range(4):
                     c = 4 * a + t
-                    nc.scalar.activation(
-                        out=hp[:, c, :], in_=zT_of[k][a][:, t, :], func=ACT.Identity,
-                        bias=gb[:, 8 + c : 9 + c], scale=gb[:, c : c + 1],
-                    )
+                    if a == 1 and k % AF_ON_VECTOR_EVERY == AF_ON_VECTOR_EVERY - 1:
+                        nc.vector.tensor_scalar(
+                            out=hp[:, c, :], in0=zT_of[k][a][:, t, :], scalar1=gb[:, c : c + 1],
+                            scalar2=gb[:, 8 + c : 9 + c], op0=ALU.mult, op1=ALU.add,
+                        )
+                    else:
+                        nc.scalar.activation(
+                            out=hp[:, c, :], in_=zT_of[k][a][:, t, :], func=ACT.Identity,
+                            bias=gb[:, 8 + c : 9 + c], scale=gb[:, c : c + 1],
+                        )
             hp_of[k] = hp
 
         def rg(k):
@@ -250,8 +264,8 @@ def tile_mldecoder_pb_t_kernel(tc, ff_hid, tgt, w2, b2, g3, be3, dup_pool, dup_b
             dg_of[k] = dg
 
         def qd(k):
-            dc = work.tile([P, 2 * G], U32, tag="dc", bufs=8, align_bytes=64)
-            ds = work.tile([P, 2 * G], U8, tag="ds", bufs=8, align_bytes=64)
+            dc = work.tile([P, 2 * G], U32, tag="dc", bufs=6, align_bytes=64)
+            ds = work.tile([P, 2 * G], U8, tag="ds", bufs=6, align_bytes=64)
             nc.vector.quantize_mx(
                 out=dc[:].bitcast(FP8X4), scales=ds[:], in_=dg_of[k][:].rearrange("p a g t -> p (a g t)")
             )
@@ -284,13 +298,21 @@ def tile_mldecoder_pb_t_kernel(tc, ff_hid, tgt, w2, b2, g3, be3, dup_pool, dup_b
         def tok(k):
             return 0 <= k < K
 
-        for n in range(-4, K + 7):
+        gain_shift_columns()
+        t_ff(0)
+        c_ff(0)
+        q_ff(0)
+        regroup_w2()
+        quant_w2(0)
+        for n in range(-3, K + 7):
             if n % 2 == 0:
                 p_new = (n + 8) // 2
                 if 3 <= p_new < K // 2:
                     load_ffh(p_new)
                     load_tgt(p_new)
                     load_dup(p_new)
+            if n == 0:
+                nc.sync.dma_start(out=dbias[:], in_=dup_bias.partition_broadcast(P))
             if tok(n):
                 p1(n)
                 nm(n)
@@ -306,14 +328,13 @@ def tile_mldecoder_pb_t_kernel(tc, ff_hid, tgt, w2, b2, g3, be3, dup_pool, dup_b
                 m2(n - 5)
             if tok(n - 3):
                 af(n - 3)
-            if n == -4:
-                quant_w2(0)
-                quant_w2(1)
             if tok(n + 2):
                 tb(n + 2)
+            if n == -2:
+                quant_w2(1)
             if tok(n - 2):
                 tz(n - 2)
-            if (n + 2) % 2 == 0 and tok(n + 2):
+            if n >= 0 and n % 2 == 0 and tok(n + 2):
                 q_ff((n + 2) // 2)
             if tok(n - 4):
                 qh(n - 4)
@@ -323,13 +344,11 @@ def tile_mldecoder_pb_t_kernel(tc, ff_hid, tgt, w2, b2, g3, be3, dup_pool, dup_b
                 sq(n)
             if tok(n - 1):
                 nbias(n - 1)
-            if tok(n + 1):
-                qd(n + 1)
-            if tok(n + 3):
-                dr(n + 3)
-            if (n + 4) % 2 == 0 and tok(n + 4):
+            if tok(n - 2):
+                qd(n - 2)
+            if tok(n):
+                dr(n)
+            if n >= -2 and n % 2 == 0 and tok(n + 4):
                 t_ff((n + 4) // 2)
-            if (n + 3) % 2 == 0 and tok(n + 3):
+            if n >= -1 and (n + 3) % 2 == 0 and tok(n + 3):
                 c_ff((n + 3) // 2)
-            if n == -1:
-                gain_shift_columns()

@@ -17,7 +17,7 @@ EPS = 1e-5
 FLOPS = 2 * B * K * FF * D + 2 * B * K * D * G
 DUP_ON_GPSIMD = True
 XH_ON_VECTOR_FROM = K
-AF_ON_VECTOR_EVERY = 4
+AF_ON_VECTOR_EVERY = 64
 
 
 def tile_mldecoder_pb_t_kernel(tc, ff_hid, tgt, w2, b2, g3, be3, dup_pool, dup_bias, out):
@@ -26,7 +26,7 @@ def tile_mldecoder_pb_t_kernel(tc, ff_hid, tgt, w2, b2, g3, be3, dup_pool, dup_b
         const = ctx.enter_context(tc.tile_pool(name="const", bufs=1))
         loads = ctx.enter_context(tc.tile_pool(name="loads", bufs=5))
         work = ctx.enter_context(tc.tile_pool(name="work", bufs=2))
-        small = ctx.enter_context(tc.tile_pool(name="small", bufs=6))
+        small = ctx.enter_context(tc.tile_pool(name="small", bufs=8))
         psum = ctx.enter_context(tc.psum_pool(name="psum", bufs=2))
         ctx.enter_context(tc.manual_schedule())
 
@@ -76,7 +76,7 @@ def tile_mldecoder_pb_t_kernel(tc, ff_hid, tgt, w2, b2, g3, be3, dup_pool, dup_b
         eps_t = const.tile([P, 1], F32)
         nc.vector.memset(eps_t[:], EPS)
         warm = const.tile([P, 1], F32)
-        nc.scalar.activation(out=warm[:], in_=eps_t[:], func=ACT.Sqrt)
+        nc.scalar.activation(out=warm[:], in_=eps_t[:], func=ACT.Abs_reciprocal_sqrt)
         ident_f = const.tile([P, P], F32)
         make_identity(nc, ident_f[:])
         ident_b = const.tile([P, P], BF16)
@@ -133,7 +133,7 @@ def tile_mldecoder_pb_t_kernel(tc, ff_hid, tgt, w2, b2, g3, be3, dup_pool, dup_b
             ff_q[p] = (ffc, ffs)
 
         def tb(k):
-            u_t = work.tile([P, D], F32, tag="u", bufs=6)
+            u_t = work.tile([P, D], F32, tag="u", bufs=7)
             nc.vector.tensor_tensor(out=u_t[:], in0=tgt_t[k // 2][:, k % 2, :], in1=b2bc[:], op=ALU.add)
             u_of[k] = u_t
 
@@ -180,13 +180,13 @@ def tile_mldecoder_pb_t_kernel(tc, ff_hid, tgt, w2, b2, g3, be3, dup_pool, dup_b
             nc.scalar.activation(
                 out=junk[:], in_=u_of[k][:], func=ACT.Square, bias=negm_of[k][:], scale=1.0, accum_out=ss[:]
             )
-            std = small.tile([P, 1], F32, tag="std")
-            nc.scalar.activation(out=std[:], in_=ss[:], func=ACT.Sqrt, bias=eps_t[:], scale=1.0 / D)
-            std_of[k] = std
+            ss_of[k] = ss
 
-        def rc(k):
+        def sr(k):
             rstd = small.tile([P, 1], F32, tag="rstd")
-            nc.vector.reciprocal(out=rstd[:], in_=std_of[k][:])
+            nc.scalar.activation(
+                out=rstd[:], in_=ss_of[k][:], func=ACT.Abs_reciprocal_sqrt, bias=eps_t[:], scale=1.0 / D
+            )
             rstd_of[k] = rstd
 
         def nbias(k):
@@ -216,22 +216,16 @@ def tile_mldecoder_pb_t_kernel(tc, ff_hid, tgt, w2, b2, g3, be3, dup_pool, dup_b
                 banks.append(zT)
             zT_of[k] = banks
 
-        def af(k):
-            hp = work.tile([P, 8, P], BF16, tag="hp", bufs=2)
-            for a in range(2):
-                for t in range(4):
-                    c = 4 * a + t
-                    if a == 1 and k % AF_ON_VECTOR_EVERY == AF_ON_VECTOR_EVERY - 1:
-                        nc.vector.tensor_scalar(
-                            out=hp[:, c, :], in0=zT_of[k][a][:, t, :], scalar1=gb[:, c : c + 1],
-                            scalar2=gb[:, 8 + c : 9 + c], op0=ALU.mult, op1=ALU.add,
-                        )
-                    else:
-                        nc.scalar.activation(
-                            out=hp[:, c, :], in_=zT_of[k][a][:, t, :], func=ACT.Identity,
-                            bias=gb[:, 8 + c : 9 + c], scale=gb[:, c : c + 1],
-                        )
-            hp_of[k] = hp
+        def af(k, a):
+            if a == 0:
+                hp_new = work.tile([P, 8, P], BF16, tag="hp", bufs=2)
+                hp_of[k] = hp_new
+            for t in range(4):
+                c = 4 * a + t
+                nc.scalar.activation(
+                    out=hp_of[k][:, c, :], in_=zT_of[k][a][:, t, :], func=ACT.Identity,
+                    bias=gb[:, 8 + c : 9 + c], scale=gb[:, c : c + 1],
+                )
 
         def rg(k):
             hg = work.tile([P, 2, P, 4], BF16, tag="hg", bufs=3, align_bytes=64)
@@ -304,7 +298,7 @@ def tile_mldecoder_pb_t_kernel(tc, ff_hid, tgt, w2, b2, g3, be3, dup_pool, dup_b
         q_ff(0)
         regroup_w2()
         quant_w2(0)
-        for n in range(-3, K + 7):
+        for n in range(-3, K + 8):
             if n % 2 == 0:
                 p_new = (n + 8) // 2
                 if 3 <= p_new < K // 2:
@@ -315,35 +309,38 @@ def tile_mldecoder_pb_t_kernel(tc, ff_hid, tgt, w2, b2, g3, be3, dup_pool, dup_b
                 nc.sync.dma_start(out=dbias[:], in_=dup_bias.partition_broadcast(P))
             if tok(n):
                 p1(n)
-                nm(n)
-            if tok(n - 1):
-                rc(n - 1)
-            if tok(n - 6) and (n - 6) % 4 == 3:
-                oa((n - 6) // 4)
+            if tok(n - 7) and (n - 7) % 4 == 3:
+                oa((n - 7) // 4)
+            if tok(n - 4):
+                af(n - 4, 0)
+            if tok(n - 3):
+                xh(n - 3)
             if tok(n - 2):
-                xh(n - 2)
+                sr(n - 2)
             if tok(n + 1):
                 m1(n + 1)
-            if tok(n - 5):
-                m2(n - 5)
-            if tok(n - 3):
-                af(n - 3)
+            if tok(n - 6):
+                m2(n - 6)
+            if tok(n - 4):
+                af(n - 4, 1)
             if tok(n + 2):
                 tb(n + 2)
             if n == -2:
                 quant_w2(1)
-            if tok(n - 2):
-                tz(n - 2)
+            if tok(n):
+                nm(n)
+            if tok(n - 3):
+                tz(n - 3)
             if n >= 0 and n % 2 == 0 and tok(n + 2):
                 q_ff((n + 2) // 2)
+            if tok(n - 5):
+                qh(n - 5)
             if tok(n - 4):
-                qh(n - 4)
-            if tok(n - 3):
-                rg(n - 3)
-            if tok(n):
-                sq(n)
+                rg(n - 4)
             if tok(n - 1):
-                nbias(n - 1)
+                sq(n - 1)
+            if tok(n - 2):
+                nbias(n - 2)
             if tok(n - 2):
                 qd(n - 2)
             if tok(n):

from contextlib import ExitStack

import concourse.mybir as mybir
from concourse.masks import make_identity

F32 = mybir.dt.float32
BF16 = mybir.dt.bfloat16
U32 = mybir.dt.uint32
U8 = mybir.dt.uint8
FP8X4 = mybir.dt.float8_e4m3fn_x4
ALU = mybir.AluOpType
ACT = mybir.ActivationFunctionType

P = 128
B, K, G, D, FF = 128, 32, 128, 1024, 512
EPS = 1e-5
FLOPS = 2 * B * K * FF * D + 2 * B * K * D * G
DUP_ON_GPSIMD = True
XH_ON_VECTOR_FROM = K
AF_ON_VECTOR_EVERY = 64


def tile_mldecoder_pb_t_kernel(tc, ff_hid, tgt, w2, b2, g3, be3, dup_pool, dup_bias, out):
    nc = tc.nc
    with ExitStack() as ctx:
        const = ctx.enter_context(tc.tile_pool(name="const", bufs=1))
        loads = ctx.enter_context(tc.tile_pool(name="loads", bufs=5))
        work = ctx.enter_context(tc.tile_pool(name="work", bufs=2))
        small = ctx.enter_context(tc.tile_pool(name="small", bufs=8))
        psum = ctx.enter_context(tc.psum_pool(name="psum", bufs=2))
        ctx.enter_context(tc.manual_schedule())

        ffh_t, tgt_t, dup_t = {}, {}, {}
        ffT_t, ffg_t, ff_q = {}, {}, {}
        u_of, s1_of, s0_of, negm_of, ss_of, std_of, rstd_of, nb_of = {}, {}, {}, {}, {}, {}, {}, {}
        z_of, zT_of, hp_of, hg_of, h_q, dg_of, d_q, o2_t = {}, {}, {}, {}, {}, {}, {}, {}

        def load_ffh(p):
            ffh = loads.tile([P, 2, FF], BF16, tag="ffh", bufs=4)
            nc.sync.dma_start(out=ffh[:], in_=ff_hid[:, 2 * p : 2 * p + 2, :])
            ffh_t[p] = ffh

        def load_tgt(p):
            tg = loads.tile([P, 2, D], BF16, tag="tg", bufs=5)
            nc.sync.dma_start(out=tg[:], in_=tgt[:, 2 * p : 2 * p + 2, :])
            tgt_t[p] = tg

        def load_dup(p):
            dr_t = loads.tile([P, 2, 8, G], BF16, tag="dr", bufs=5)
            nc.sync.dma_start(out=dr_t[:], in_=dup_pool[2 * p : 2 * p + 2].rearrange("k (c p) g -> p k c g", p=P))
            dup_t[p] = dr_t

        gb_raw = const.tile([P, P], BF16)
        nc.vector.memset(gb_raw[:], 0.0)
        nc.sync.dma_start(out=gb_raw[0:8, :], in_=g3.rearrange("(c p) -> c p", p=P))
        nc.sync.dma_start(out=gb_raw[8:16, :], in_=be3.rearrange("(c p) -> c p", p=P))
        load_ffh(0)
        w2raw = const.tile([P, 4, D], BF16)
        for u in range(2):
            nc.sync.dma_start(
                out=w2raw[:, 2 * u : 2 * u + 2, :],
                in_=w2[256 * u : 256 * u + 256, :].rearrange("(q e) c -> q e c", e=2),
            )
        b2bc = const.tile([P, D], BF16)
        nc.sync.dma_start(out=b2bc[:], in_=b2.partition_broadcast(P))
        load_tgt(0)
        load_ffh(1)
        load_tgt(1)
        load_dup(0)
        load_dup(1)
        load_ffh(2)
        load_tgt(2)
        load_dup(2)
        dbias = const.tile([P, K * G], BF16)

        eps_t = const.tile([P, 1], F32)
        nc.vector.memset(eps_t[:], EPS)
        warm = const.tile([P, 1], F32)
        nc.scalar.activation(out=warm[:], in_=eps_t[:], func=ACT.Abs_reciprocal_sqrt)
        ident_f = const.tile([P, P], F32)
        make_identity(nc, ident_f[:])
        ident_b = const.tile([P, P], BF16)
        make_identity(nc, ident_b[:])

        w2c = const.tile([P, D], U32, align_bytes=64)
        w2s = const.tile([P, D], U8, align_bytes=64)
        w2g = const.tile([P, 2, 512, 4], BF16, align_bytes=64)

        def regroup_w2():
            nc.vector.tensor_copy(
                out=w2g[:, 0].rearrange("p (c i) t -> p c t i", i=4),
                in_=w2raw[:, :, 0:512].rearrange("p t (c i) -> p c t i", i=4),
            )
            nc.scalar.copy(
                out=w2g[:, 1].rearrange("p (c i) t -> p c t i", i=4),
                in_=w2raw[:, :, 512:1024].rearrange("p t (c i) -> p c t i", i=4),
            )

        def quant_w2(h):
            nc.vector.quantize_mx(
                out=w2c[:, 512 * h : 512 * h + 512].bitcast(FP8X4),
                scales=w2s[:, 512 * h : 512 * h + 512],
                in_=w2g[:, h].rearrange("p c t -> p (c t)"),
            )

        gb = const.tile([P, 16], F32)

        def gain_shift_columns():
            gb_ps = psum.tile([P, P], BF16, tag="o2", bufs=2)
            nc.tensor.transpose(gb_ps[:], gb_raw[:], ident_b[:])
            nc.vector.tensor_copy(out=gb[:], in_=gb_ps[:, 0:16])

        def t_ff(p):
            ffT = psum.tile([P, 2, 2, P], F32, tag="ffT", bufs=1)
            for j in range(2):
                k = 2 * p + j
                words = ffh_t[p][:, j, :].bitcast(F32)
                for u in range(2):
                    nc.tensor.transpose(ffT[:, j, u, :], words[:, P * u : P * u + P], ident_f[:])
            ffT_t[p] = ffT

        def c_ff(p):
            ffg = work.tile([P, 2, P, 4], BF16, tag="ffg", bufs=2, align_bytes=64)
            nc.scalar.copy(out=ffg[:].bitcast(F32), in_=ffT_t[p][:].rearrange("p j u b -> p j b u"))
            ffg_t[p] = ffg

        def q_ff(p):
            ffc = work.tile([P, 2 * P], U32, tag="ffc", bufs=3, align_bytes=64)
            ffs = work.tile([P, 2 * P], U8, tag="ffs", bufs=3, align_bytes=64)
            nc.vector.quantize_mx(
                out=ffc[:].bitcast(FP8X4), scales=ffs[:], in_=ffg_t[p][:].rearrange("p j b t -> p (j b t)")
            )
            ff_q[p] = (ffc, ffs)

        def tb(k):
            u_t = work.tile([P, D], F32, tag="u", bufs=7)
            nc.vector.tensor_tensor(out=u_t[:], in0=tgt_t[k // 2][:, k % 2, :], in1=b2bc[:], op=ALU.add)
            u_of[k] = u_t

        def m1(k):
            ffc, ffs = ff_q[k // 2]
            cols = slice(P * (k % 2), P * (k % 2) + P)
            banks = []
            for h in range(2):
                s1 = psum.tile([P, 512], F32, tag="s1", bufs=3)
                n_cols = slice(512 * h, 512 * h + 512)
                nc.tensor.matmul_mx(
                    out=s1[:],
                    lhsT=ffc[:, cols].bitcast(FP8X4),
                    lhsT_scale=ffs[:, cols],
                    rhs=w2c[:, n_cols].bitcast(FP8X4),
                    rhs_scale=w2s[:, n_cols],
                    start=True,
                    stop=True,
                )
                banks.append(s1)
            s1_of[k] = banks

        def p1(k):
            s0 = small.tile([P, 2], F32, tag="s0")
            for h in range(2):
                n_cols = slice(512 * h, 512 * h + 512)
                nc.vector.scalar_tensor_tensor(
                    out=u_of[k][:, n_cols], in0=s1_of[k][h][:], scalar=1.0, in1=u_of[k][:, n_cols],
                    op0=ALU.mult, op1=ALU.add, accum_out=s0[:, h : h + 1],
                )
            s0_of[k] = s0

        def nm(k):
            negm = small.tile([P, 1], F32, tag="negm")
            s0 = s0_of[k]
            nc.vector.tensor_scalar(
                out=negm[:], in0=s0[:, 0:1], scalar1=s0[:, 1:2], scalar2=-1.0 / D, op0=ALU.add, op1=ALU.mult
            )
            negm_of[k] = negm

        def sq(k):
            junk = work.tile([P, D], BF16, tag="junk", bufs=1)
            ss = small.tile([P, 1], F32, tag="ss")
            nc.scalar.activation(
                out=junk[:], in_=u_of[k][:], func=ACT.Square, bias=negm_of[k][:], scale=1.0, accum_out=ss[:]
            )
            ss_of[k] = ss

        def sr(k):
            rstd = small.tile([P, 1], F32, tag="rstd")
            nc.scalar.activation(
                out=rstd[:], in_=ss_of[k][:], func=ACT.Abs_reciprocal_sqrt, bias=eps_t[:], scale=1.0 / D
            )
            rstd_of[k] = rstd

        def nbias(k):
            nb = small.tile([P, 1], F32, tag="nb")
            nc.scalar.activation(out=nb[:], in_=negm_of[k][:], func=ACT.Copy, scale=rstd_of[k][:])
            nb_of[k] = nb

        def xh(k):
            z = work.tile([P, D], F32, tag="z", bufs=2)
            if k >= XH_ON_VECTOR_FROM:
                nc.vector.tensor_scalar(
                    out=z[:], in0=u_of[k][:], scalar1=negm_of[k][:], scalar2=rstd_of[k][:], op0=ALU.add, op1=ALU.mult
                )
            else:
                nc.scalar.activation(
                    out=z[:], in_=u_of[k][:], func=ACT.Identity, bias=nb_of[k][:], scale=rstd_of[k][:]
                )
            z_of[k] = z

        def tz(k):
            banks = []
            for a in range(2):
                zT = psum.tile([P, 4, P], F32, tag="zT", bufs=2)
                for t in range(4):
                    c = 4 * a + t
                    nc.tensor.transpose(zT[:, t, :], z_of[k][:, P * c : P * c + P], ident_f[:])
                banks.append(zT)
            zT_of[k] = banks

        def af(k, a):
            if a == 0:
                hp_new = work.tile([P, 8, P], BF16, tag="hp", bufs=2)
                hp_of[k] = hp_new
            for t in range(4):
                c = 4 * a + t
                nc.scalar.activation(
                    out=hp_of[k][:, c, :], in_=zT_of[k][a][:, t, :], func=ACT.Identity,
                    bias=gb[:, 8 + c : 9 + c], scale=gb[:, c : c + 1],
                )

        def rg(k):
            hg = work.tile([P, 2, P, 4], BF16, tag="hg", bufs=3, align_bytes=64)
            nc.vector.tensor_copy(
                out=hg[:].rearrange("p a (c i) t -> p a c t i", i=4),
                in_=hp_of[k][:].rearrange("p (a t) (c i) -> p a c t i", t=4, i=4),
            )
            hg_of[k] = hg

        def qh(k):
            hc = work.tile([P, 2 * P], U32, tag="hc", bufs=3, align_bytes=64)
            hs = work.tile([P, 2 * P], U8, tag="hs", bufs=3, align_bytes=64)
            nc.vector.quantize_mx(
                out=hc[:].bitcast(FP8X4), scales=hs[:], in_=hg_of[k][:].rearrange("p a b t -> p (a b t)")
            )
            h_q[k] = (hc, hs)

        def dr(k):
            dg = work.tile([P, 2, G, 4], BF16, tag="dg", bufs=2, align_bytes=64)
            if DUP_ON_GPSIMD:
                nc.gpsimd.tensor_scalar(
                    out=dg[:], in0=dup_t[k // 2][:, k % 2].rearrange("p (a t) g -> p a g t", t=4),
                    scalar1=1.0, scalar2=0.0, op0=ALU.mult, op1=ALU.add,
                )
            else:
                nc.vector.tensor_copy(
                    out=dg[:].rearrange("p a (c i) t -> p a c t i", i=4),
                    in_=dup_t[k // 2][:, k % 2].rearrange("p (a t) (c i) -> p a c t i", t=4, i=4),
                )
            dg_of[k] = dg

        def qd(k):
            dc = work.tile([P, 2 * G], U32, tag="dc", bufs=6, align_bytes=64)
            ds = work.tile([P, 2 * G], U8, tag="ds", bufs=6, align_bytes=64)
            nc.vector.quantize_mx(
                out=dc[:].bitcast(FP8X4), scales=ds[:], in_=dg_of[k][:].rearrange("p a g t -> p (a g t)")
            )
            d_q[k] = (dc, ds)

        def m2(k):
            if k % 4 == 0:
                o2_new = psum.tile([P, 4 * G], F32, tag="o2", bufs=2)
                o2_t[k // 4] = o2_new
            hc, hs = h_q[k]
            dc, ds = d_q[k]
            for a in range(2):
                sl = slice(P * a, P * a + P)
                nc.tensor.matmul_mx(
                    out=o2_t[k // 4][:, G * (k % 4) : G * (k % 4) + G],
                    lhsT=hc[:, sl].bitcast(FP8X4),
                    lhsT_scale=hs[:, sl],
                    rhs=dc[:, sl].bitcast(FP8X4),
                    rhs_scale=ds[:, sl],
                    start=(a == 0),
                    stop=(a == 1),
                )

        def oa(g):
            o_cols = slice(4 * G * g, 4 * G * g + 4 * G)
            ob = work.tile([P, 4 * G], F32, tag="ob", bufs=2)
            nc.vector.tensor_tensor(out=ob[:], in0=o2_t[g][:], in1=dbias[:, o_cols], op=ALU.add)
            nc.sync.dma_start(out=out[:, o_cols], in_=ob[:])

        def tok(k):
            return 0 <= k < K

        gain_shift_columns()
        t_ff(0)
        c_ff(0)
        q_ff(0)
        regroup_w2()
        quant_w2(0)
        for n in range(-3, K + 8):
            if n % 2 == 0:
                p_new = (n + 8) // 2
                if 3 <= p_new < K // 2:
                    load_ffh(p_new)
                    load_tgt(p_new)
                    load_dup(p_new)
            if n == 0:
                nc.sync.dma_start(out=dbias[:], in_=dup_bias.partition_broadcast(P))
            if tok(n):
                p1(n)
            if tok(n - 7) and (n - 7) % 4 == 3:
                oa((n - 7) // 4)
            if tok(n - 4):
                af(n - 4, 0)
            if tok(n - 3):
                xh(n - 3)
            if tok(n - 2):
                sr(n - 2)
            if tok(n + 1):
                m1(n + 1)
            if tok(n - 6):
                m2(n - 6)
            if tok(n - 4):
                af(n - 4, 1)
            if tok(n + 2):
                tb(n + 2)
            if n == -2:
                quant_w2(1)
            if tok(n):
                nm(n)
            if tok(n - 3):
                tz(n - 3)
            if n >= 0 and n % 2 == 0 and tok(n + 2):
                q_ff((n + 2) // 2)
            if tok(n - 5):
                qh(n - 5)
            if tok(n - 4):
                rg(n - 4)
            if tok(n - 1):
                sq(n - 1)
            if tok(n - 2):
                nbias(n - 2)
            if tok(n - 2):
                qd(n - 2)
            if tok(n):
                dr(n)
            if n >= -2 and n % 2 == 0 and tok(n + 4):
                t_ff((n + 4) // 2)
            if n >= -1 and (n + 3) % 2 == 0 and tok(n + 3):
                c_ff((n + 3) // 2)
